import numpy as np
import ml_dtypes


def mxq(x, axis, fmt="e4m3"):
    dtype, down = {"e4m3": (ml_dtypes.float8_e4m3fn, 7), "e5m2": (ml_dtypes.float8_e5m2, 14)}[fmt]
    v = np.moveaxis(np.asarray(x, np.float32).astype(ml_dtypes.bfloat16).astype(np.float64), axis, -1)
    blocks = v.reshape(v.shape[:-1] + (-1, 32))
    amax = np.abs(blocks).max(-1, keepdims=True)
    byte = np.maximum(np.where(amax > 0, np.frexp(amax)[1] - 1 + 127, 0) - down, 1)
    scale = np.exp2(byte - 127.0)
    codes = (blocks / scale).astype(np.float32).astype(dtype).astype(np.float64)
    return np.moveaxis((codes * scale).reshape(v.shape), -1, axis)


WIDE = False


def mx_kscale(k):
    if not WIDE:
        return np.ones(k)
    levels = np.array([10, -10, 5, -5, 0])
    a = np.random.permutation(np.resize(levels, k // 512 * 4)).reshape(k // 512, 4)
    idx = np.arange(k)
    return np.exp2(a[idx // 512, idx % 128 // 32])


BF16 = ml_dtypes.bfloat16


def bf(x):
    return np.asarray(x, np.float32).astype(BF16)


def f64(x):
    return np.asarray(x).astype(np.float64)


B, D, V, H = 256, 16, 128, 512
K = D * V
LN_EPS = 1e-5


def erf(u):
    a = np.minimum(np.abs(u), 6.0)
    q = 2.0 * a * a
    t = a.copy()
    acc = a.copy()
    for n in range(1, 101):
        t *= q
        t /= 2 * n + 1
        acc += t
    return np.sign(u) * acc * np.exp(-a * a) * 2.0 / np.sqrt(np.pi)


def gelu(u):
    return 0.5 * u * (1.0 + erf(u / np.sqrt(2.0)))


def setup_inputs():
    s = mx_kscale(K)
    return {"causal_vars": bf(np.random.standard_normal((B, D, V)) * s.reshape(D, V)),
            "adj_soft": bf(0.2 + 0.8 * np.random.random((D, D))),
            "W1": bf(np.random.standard_normal((D, K, H)) * 1.5 / np.sqrt(K) / s[None, :, None]),
            "b1": bf(np.random.standard_normal((D, H)) * 0.3),
            "W2": bf(np.random.standard_normal((D, H, V)) * 0.024 / np.sqrt(H)),
            "b2": bf(np.random.standard_normal((D, V)) * 0.006),
            "gamma": bf(1.0 + 0.1 * np.random.standard_normal((D, V))),
            "beta": bf(0.1 * np.random.standard_normal((D, V)))}


def reference(causal_vars, adj_soft, W1, b1, W2, b2, gamma, beta):
    x = f64(adj_soft)[None, :, :, None] * f64(causal_vars)[:, None, :, :]
    x = x.reshape(B, D, K)
    xq = mxq(x, 2, "e4m3")
    h = (xq.transpose(1, 0, 2) @ mxq(f64(W1), 1, "e4m3")).transpose(1, 0, 2) + f64(b1)[None]
    h = gelu(h)
    hq = mxq(h, 2, "e4m3")
    y = (hq.transpose(1, 0, 2) @ mxq(f64(W2), 1, "e4m3")).transpose(1, 0, 2) + f64(b2)[None]
    mu = np.mean(y, axis=-1, keepdims=True)
    var = np.var(y, axis=-1, keepdims=True)
    y = (y - mu) * (1.0 / np.sqrt(var + LN_EPS))
    return y * f64(gamma)[None] + f64(beta)[None]

@@ -1,0 +1,262 @@
+from contextlib import ExitStack
+
+import concourse.mybir as mybir
+from concourse.masks import make_identity
+
+FP8X4 = mybir.dt.float8_e4m3fn_x4
+BF16 = mybir.dt.bfloat16
+F32 = mybir.dt.float32
+U32 = mybir.dt.uint32
+U8 = mybir.dt.uint8
+ALU = mybir.AluOpType
+ACT = mybir.ActivationFunctionType
+
+B, D, V, H = 256, 16, 128, 512
+K = D * V
+P = 128
+PACK = 4
+K_PASS = P * PACK
+G = K // K_PASS
+C = H // P
+BC = B // P
+LN_EPS = 1e-5
+FLOPS = 2 * B * D * (K * H + H * V)
+
+SCALAR_UNITS = (0, 1, 2)
+AHEAD = 2
+
+
+def regroup(copy, dst, src):
+    copy(
+        out=dst.rearrange("p (c i) t -> p c t i", i=4),
+        in_=src.rearrange("p t (c i) -> p c t i", i=4),
+    )
+
+
+def tile_structuralequationmodels_kernel(
+    tc, causal_vars, adj_soft, W1, b1, W2, b2, gamma, beta, out
+):
+    nc = tc.nc
+    with ExitStack() as ctx:
+        const = ctx.enter_context(tc.tile_pool(name="const", bufs=1))
+        rawp = ctx.enter_context(tc.tile_pool(name="rawp", bufs=(AHEAD + 1) * G))
+        grpp = ctx.enter_context(tc.tile_pool(name="grpp", bufs=6))
+        w1qp = ctx.enter_context(tc.tile_pool(name="w1qp", bufs=3))
+        xp = ctx.enter_context(tc.tile_pool(name="xp", bufs=2))
+        xqp = ctx.enter_context(tc.tile_pool(name="xqp", bufs=3))
+        hp = ctx.enter_context(tc.tile_pool(name="hp", bufs=3))
+        lnp = ctx.enter_context(tc.tile_pool(name="lnp", bufs=4))
+        stp = ctx.enter_context(tc.tile_pool(name="stp", bufs=4))
+        ps_set = ctx.enter_context(tc.psum_pool(name="ps_set", bufs=2))
+        ps_h = ctx.enter_context(tc.psum_pool(name="ps_h", bufs=4))
+        ps_y = ctx.enter_context(tc.psum_pool(name="ps_y", bufs=2))
+
+        raws = {}
+
+        def load_w1(i, g):
+            raw = rawp.tile([P, PACK * H], BF16, name="raw")
+            nc.sync.dma_start(
+                out=raw[:],
+                in_=W1[i][g * K_PASS : (g + 1) * K_PASS, :].rearrange("(p t) h -> p (t h)", t=PACK),
+            )
+            raws[(i, g)] = raw
+
+        load_w1(0, 0)
+        cvr = const.tile([P, BC, K], BF16, name="cvr")
+        nc.sync.dma_start(out=cvr[:], in_=causal_vars.rearrange("(c p) j v -> p c (j v)", p=P))
+        adjb = const.tile([P, D * D], BF16, name="adjb")
+        nc.sync.dma_start(out=adjb[:], in_=adj_soft.rearrange("i j -> (i j)").partition_broadcast(P))
+        b1t = const.tile([P, P], BF16, name="b1t")
+        nc.vector.memset(b1t[:], 0.0)
+        nc.sync.dma_start(out=b1t[0 : D * C, :], in_=b1.rearrange("i (c m) -> (i c) m", m=P))
+        for g in range(1, G):
+            load_w1(0, g)
+        w2r = const.tile([P, D, PACK, V], BF16, name="w2r")
+        nc.sync.dma_start(out=w2r[:, 0:4], in_=W2[0:4].rearrange("i (t p) v -> p i t v", p=P))
+        for g in range(G):
+            load_w1(1, g)
+        b2bc = const.tile([P, D * V], BF16, name="b2bc")
+        nc.sync.dma_start(out=b2bc[:], in_=b2.rearrange("i v -> (i v)").partition_broadcast(P))
+        gbc = const.tile([P, D * V], BF16, name="gbc")
+        nc.sync.dma_start(out=gbc[:], in_=gamma.rearrange("i v -> (i v)").partition_broadcast(P))
+        bbc = const.tile([P, D * V], BF16, name="bbc")
+        nc.sync.dma_start(out=bbc[:], in_=beta.rearrange("i v -> (i v)").partition_broadcast(P))
+        for q in range(1, 4):
+            nc.sync.dma_start(
+                out=w2r[:, 4 * q : 4 * q + 4],
+                in_=W2[4 * q : 4 * q + 4].rearrange("i (t p) v -> p i t v", p=P),
+            )
+
+        ident_f = const.tile([P, P], F32, name="ident_f")
+        make_identity(nc, ident_f[:])
+        ident_b = const.tile([P, P], BF16, name="ident_b")
+        make_identity(nc, ident_b[:])
+        negh = const.tile([P, BC], F32, name="negh")
+        nc.vector.memset(negh[:], -0.5)
+
+        adjcol = const.tile([P, D * G], F32, name="adjcol")
+        for q in range(4):
+            rows = slice(32 * q, 32 * q + 32)
+            nc.vector.tensor_copy(
+                out=adjcol[rows, :].rearrange("p (i g) -> p i g", g=G),
+                in_=adjb[rows, :].rearrange("p (i g q) -> p i g q", g=G, q=4)[:, :, :, q],
+            )
+
+        b1ps = ps_set.tile([P, P], BF16, name="b1ps", tag="set")
+        nc.tensor.transpose(b1ps[:], b1t[:], ident_b[:])
+        b1col = const.tile([P, D * C], F32, name="b1col")
+        nc.vector.tensor_copy(out=b1col[:], in_=b1ps[:, 0 : D * C])
+
+        cvg = const.tile([P, G, B, PACK], BF16, name="cvg", align_bytes=64)
+        cvw = cvr[:].bitcast(F32)
+        cvgw = cvg[:].bitcast(F32)
+        for g in range(G):
+            xt = ps_set.tile([P, 2, B], F32, name="xt", tag="set")
+            for u in range(2):
+                for bc in range(BC):
+                    nc.tensor.transpose(
+                        xt[:, u, bc * P : (bc + 1) * P],
+                        cvw[:, bc, 256 * g + u : 256 * (g + 1) : 2],
+                        ident_f[:],
+                    )
+            nc.vector.tensor_copy(out=cvgw[:, g], in_=xt[:].rearrange("p u b -> p b u"))
+
+        out_v = out.rearrange("(c p) i v -> p c i v", p=P)
+
+        for i in range(D):
+            if i + AHEAD < D:
+                for g in range(G):
+                    load_w1(i + AHEAD, g)
+
+            xs = xp.tile([P, G, B * PACK], BF16, name="xs", align_bytes=64)
+            for g in range(G):
+                nc.vector.tensor_scalar(
+                    out=xs[:, g, :],
+                    in0=cvg[:, g].rearrange("p b t -> p (b t)"),
+                    scalar1=adjcol[:, G * i + g : G * i + g + 1],
+                    scalar2=None,
+                    op0=ALU.mult,
+                )
+            xc = xqp.tile([P, G * B], U32, name="xc", align_bytes=64)
+            xsc = xqp.tile([P, G * B], U8, name="xsc", align_bytes=64)
+            nc.vector.quantize_mx(
+                out=xc[:].bitcast(FP8X4), scales=xsc[:], in_=xs[:].rearrange("p g e -> p (g e)")
+            )
+
+            w1c = w1qp.tile([P, G, H], U32, name="w1c", align_bytes=64)
+            w1s = w1qp.tile([P, G, H], U8, name="w1s", align_bytes=64)
+            for g in range(G):
+                grp = grpp.tile([P, H, PACK], BF16, name="grp", align_bytes=64)
+                copy = nc.scalar.copy if g in SCALAR_UNITS else nc.vector.tensor_copy
+                regroup(copy, grp[:], raws[(i, g)][:].rearrange("p (t h) -> p t h", t=PACK))
+                nc.vector.quantize_mx(
+                    out=w1c[:, g, :].bitcast(FP8X4),
+                    scales=w1s[:, g, :],
+                    in_=grp[:].rearrange("p w t -> p (w t)"),
+                )
+
+            g2 = hp.tile([P, V, PACK], BF16, name="g2", align_bytes=64)
+            regroup(nc.vector.tensor_copy, g2[:], w2r[:, i])
+            w2c = hp.tile([P, V], U32, name="w2c", align_bytes=64)
+            w2s = hp.tile([P, V], U8, name="w2s", align_bytes=64)
+            nc.vector.quantize_mx(
+                out=w2c[:].bitcast(FP8X4), scales=w2s[:], in_=g2[:].rearrange("p w t -> p (w t)")
+            )
+
+            ht = hp.tile([P, C, B], BF16, name="ht")
+            for cp in range(C // 2):
+                hps = ps_h.tile([P, 2, B], F32, name="hps")
+                for cc in range(2):
+                    c = 2 * cp + cc
+                    for g in range(G):
+                        nc.tensor.matmul_mx(
+                            out=hps[:, cc, :],
+                            lhsT=w1c[:, g, c * P : (c + 1) * P].bitcast(FP8X4),
+                            lhsT_scale=w1s[:, g, c * P : (c + 1) * P],
+                            rhs=xc[:, g * B : (g + 1) * B].bitcast(FP8X4),
+                            rhs_scale=xsc[:, g * B : (g + 1) * B],
+                            start=(g == 0),
+                            stop=(g == G - 1),
+                        )
+                for cc in range(2):
+                    c = 2 * cp + cc
+                    nc.scalar.activation(
+                        out=ht[:, c, :],
+                        in_=hps[:, cc, :],
+                        func=ACT.Gelu,
+                        bias=b1col[:, C * i + c : C * i + c + 1],
+                        scale=1.0,
+                    )
+            hg = hp.tile([P, B, PACK], BF16, name="hg", align_bytes=64)
+            regroup(nc.vector.tensor_copy, hg[:], ht[:])
+            hc = hp.tile([P, B], U32, name="hc", align_bytes=64)
+            hs = hp.tile([P, B], U8, name="hs", align_bytes=64)
+            nc.vector.quantize_mx(
+                out=hc[:].bitcast(FP8X4), scales=hs[:], in_=hg[:].rearrange("p w t -> p (w t)")
+            )
+
+            yps = ps_y.tile([P, BC, V], F32, name="yps")
+            for bc in range(BC):
+                nc.tensor.matmul_mx(
+                    out=yps[:, bc, :],
+                    lhsT=hc[:, bc * P : (bc + 1) * P].bitcast(FP8X4),
+                    lhsT_scale=hs[:, bc * P : (bc + 1) * P],
+                    rhs=w2c[:].bitcast(FP8X4),
+                    rhs_scale=w2s[:],
+                    start=True,
+                    stop=True,
+                )
+
+            cols = slice(i * V, (i + 1) * V)
+            z = lnp.tile([P, BC, V], F32, name="z")
+            sz = stp.tile([P, BC], F32, name="sz")
+            for bc in range(BC):
+                nc.vector.scalar_tensor_tensor(
+                    out=z[:, bc, :],
+                    in0=yps[:, bc, :],
+                    scalar=1.0,
+                    in1=b2bc[:, cols],
+                    op0=ALU.mult,
+                    op1=ALU.add,
+                    accum_out=sz[:, bc : bc + 1],
+                )
+            nm = stp.tile([P, BC], F32, name="nm")
+            nc.vector.tensor_scalar(out=nm[:], in0=sz[:], scalar1=-1.0 / V, scalar2=None, op0=ALU.mult)
+            ssq = stp.tile([P, BC], F32, name="ssq")
+            for bc in range(BC):
+                junk = lnp.tile([P, V], F32, name="junk")
+                nc.scalar.activation(
+                    out=junk[:],
+                    in_=z[:, bc, :],
+                    func=ACT.Square,
+                    bias=nm[:, bc : bc + 1],
+                    scale=1.0,
+                    accum_out=ssq[:, bc : bc + 1],
+                )
+            ve = stp.tile([P, BC], F32, name="ve")
+            nc.gpsimd.tensor_scalar(
+                out=ve[:], in0=ssq[:], scalar1=1.0 / V, scalar2=LN_EPS, op0=ALU.mult, op1=ALU.add
+            )
+            rstd = stp.tile([P, BC], F32, name="rstd")
+            nc.gpsimd.tensor_tensor(out=rstd[:], in0=ve[:], in1=negh[:], op=ALU.pow)
+            tt = lnp.tile([P, BC, V], F32, name="tt")
+            o = lnp.tile([P, BC, V], F32, name="o")
+            for bc in range(BC):
+                nc.vector.scalar_tensor_tensor(
+                    out=tt[:, bc, :],
+                    in0=z[:, bc, :],
+                    scalar=nm[:, bc : bc + 1],
+                    in1=gbc[:, cols],
+                    op0=ALU.add,
+                    op1=ALU.mult,
+                )
+            for bc in range(BC):
+                nc.vector.scalar_tensor_tensor(
+                    out=o[:, bc, :],
+                    in0=tt[:, bc, :],
+                    scalar=rstd[:, bc : bc + 1],
+                    in1=bbc[:, cols],
+                    op0=ALU.mult,
+                    op1=ALU.add,
+                )
+            nc.sync.dma_start(out=out_v[:, :, i, :], in_=o[:])

@@ -22,8 +22,9 @@ BC = B // P
 LN_EPS = 1e-5
 FLOPS = 2 * B * D * (K * H + H * V)
 
-SCALAR_UNITS = (0, 1, 2)
 AHEAD = 2
+UA, UV, UB, UC = 0, 1, 2, 3
+PASS_ORDER = (UA, UB, UV, UC)
 
 
 def regroup(copy, dst, src):
@@ -45,47 +46,229 @@ def tile_structuralequationmodels_kernel(
         xp = ctx.enter_context(tc.tile_pool(name="xp", bufs=2))
         xqp = ctx.enter_context(tc.tile_pool(name="xqp", bufs=3))
         hp = ctx.enter_context(tc.tile_pool(name="hp", bufs=3))
-        lnp = ctx.enter_context(tc.tile_pool(name="lnp", bufs=4))
+        lnp = ctx.enter_context(tc.tile_pool(name="lnp", bufs=3))
         stp = ctx.enter_context(tc.tile_pool(name="stp", bufs=4))
         ps_set = ctx.enter_context(tc.psum_pool(name="ps_set", bufs=2))
-        ps_h = ctx.enter_context(tc.psum_pool(name="ps_h", bufs=4))
+        ps_h = ctx.enter_context(tc.psum_pool(name="ps_h", bufs=1))
         ps_y = ctx.enter_context(tc.psum_pool(name="ps_y", bufs=2))
+        ctx.enter_context(tc.manual_schedule())
 
-        raws = {}
+        T = {}
+        out_v = out.rearrange("(c p) i v -> p c i v", p=P)
 
-        def load_w1(i, g):
+        def load_w1(e, g):
             raw = rawp.tile([P, PACK * H], BF16, name="raw")
             nc.sync.dma_start(
                 out=raw[:],
-                in_=W1[i][g * K_PASS : (g + 1) * K_PASS, :].rearrange("(p t) h -> p (t h)", t=PACK),
+                in_=W1[e][g * K_PASS : (g + 1) * K_PASS, :].rearrange("(p t) h -> p (t h)", t=PACK),
             )
-            raws[(i, g)] = raw
+            T[("raw", e, g)] = raw
 
-        load_w1(0, 0)
+        def w1_regroup(e, g, copy):
+            grp = grpp.tile([P, H, PACK], BF16, name="grp", align_bytes=64)
+            regroup(copy, grp[:], T[("raw", e, g)][:].rearrange("p (t h) -> p t h", t=PACK))
+            T[("grp", e, g)] = grp
+
+        def w1_quant(e, g):
+            if g == PASS_ORDER[0]:
+                T[("w1c", e)] = w1qp.tile([P, G, H], U32, name="w1c", align_bytes=64)
+                T[("w1s", e)] = w1qp.tile([P, G, H], U8, name="w1s", align_bytes=64)
+            nc.vector.quantize_mx(
+                out=T[("w1c", e)][:, g, :].bitcast(FP8X4),
+                scales=T[("w1s", e)][:, g, :],
+                in_=T[("grp", e, g)][:].rearrange("p w t -> p (w t)"),
+            )
+
+        def x_scale(e):
+            xs = xp.tile([P, G, B * PACK], BF16, name="xs", align_bytes=64)
+            for g in range(G):
+                nc.vector.tensor_scalar(
+                    out=xs[:, g, :],
+                    in0=cvg[:, g].rearrange("p b t -> p (b t)"),
+                    scalar1=adjcol[:, G * e + g : G * e + g + 1],
+                    scalar2=None,
+                    op0=ALU.mult,
+                )
+            T[("xs", e)] = xs
+
+        def x_quant(e):
+            T[("xc", e)] = xqp.tile([P, G * B], U32, name="xc", align_bytes=64)
+            T[("xsc", e)] = xqp.tile([P, G * B], U8, name="xsc", align_bytes=64)
+            nc.vector.quantize_mx(
+                out=T[("xc", e)][:].bitcast(FP8X4),
+                scales=T[("xsc", e)][:],
+                in_=T[("xs", e)][:].rearrange("p g e -> p (g e)"),
+            )
+
+        def mm1(e, g):
+            first = g == PASS_ORDER[0]
+            last = g == PASS_ORDER[-1]
+            for c in range(C):
+                if first:
+                    T[("hps", e, c)] = ps_h.tile([P, B], F32, name="hps%d" % c)
+                nc.tensor.matmul_mx(
+                    out=T[("hps", e, c)][:],
+                    lhsT=T[("w1c", e)][:, g, c * P : (c + 1) * P].bitcast(FP8X4),
+                    lhsT_scale=T[("w1s", e)][:, g, c * P : (c + 1) * P],
+                    rhs=T[("xc", e)][:, g * B : (g + 1) * B].bitcast(FP8X4),
+                    rhs_scale=T[("xsc", e)][:, g * B : (g + 1) * B],
+                    start=first,
+                    stop=last,
+                )
+
+        def gelu(e):
+            ht = hp.tile([P, C, B], BF16, name="ht")
+            for c in range(C):
+                nc.scalar.activation(
+                    out=ht[:, c, :],
+                    in_=T[("hps", e, c)][:],
+                    func=ACT.Gelu,
+                    bias=b1col[:, C * e + c : C * e + c + 1],
+                    scale=1.0,
+                )
+            T[("ht", e)] = ht
+
+        def h_regroup(e):
+            hg = hp.tile([P, B, PACK], BF16, name="hg", align_bytes=64)
+            regroup(nc.vector.tensor_copy, hg[:], T[("ht", e)][:])
+            T[("hg", e)] = hg
+
+        def h_quant(e):
+            T[("hc", e)] = hp.tile([P, B], U32, name="hc", align_bytes=64)
+            T[("hs", e)] = hp.tile([P, B], U8, name="hs", align_bytes=64)
+            nc.vector.quantize_mx(
+                out=T[("hc", e)][:].bitcast(FP8X4),
+                scales=T[("hs", e)][:],
+                in_=T[("hg", e)][:].rearrange("p w t -> p (w t)"),
+            )
+
+        def w2_regroup(e):
+            g2 = hp.tile([P, V, PACK], BF16, name="g2", align_bytes=64)
+            regroup(nc.vector.tensor_copy, g2[:], w2r[:, e])
+            T[("g2", e)] = g2
+
+        def w2_quant(e):
+            T[("w2c", e)] = hp.tile([P, V], U32, name="w2c", align_bytes=64)
+            T[("w2s", e)] = hp.tile([P, V], U8, name="w2s", align_bytes=64)
+            nc.vector.quantize_mx(
+                out=T[("w2c", e)][:].bitcast(FP8X4),
+                scales=T[("w2s", e)][:],
+                in_=T[("g2", e)][:].rearrange("p w t -> p (w t)"),
+            )
+
+        def mm2(e):
+            yps = ps_y.tile([P, BC, V], F32, name="yps")
+            for bc in range(BC):
+                nc.tensor.matmul_mx(
+                    out=yps[:, bc, :],
+                    lhsT=T[("hc", e)][:, bc * P : (bc + 1) * P].bitcast(FP8X4),
+                    lhsT_scale=T[("hs", e)][:, bc * P : (bc + 1) * P],
+                    rhs=T[("w2c", e)][:].bitcast(FP8X4),
+                    rhs_scale=T[("w2s", e)][:],
+                    start=True,
+                    stop=True,
+                )
+            T[("yps", e)] = yps
+
+        def ln_mean(e):
+            z = lnp.tile([P, BC, V], F32, name="z")
+            sz = stp.tile([P, BC], F32, name="sz")
+            for bc in range(BC):
+                nc.vector.scalar_tensor_tensor(
+                    out=z[:, bc, :],
+                    in0=T[("yps", e)][:, bc, :],
+                    scalar=1.0,
+                    in1=b2bc[:, e * V : (e + 1) * V],
+                    op0=ALU.mult,
+                    op1=ALU.add,
+                    accum_out=sz[:, bc : bc + 1],
+                )
+            nm = stp.tile([P, BC], F32, name="nm")
+            nc.vector.tensor_scalar(out=nm[:], in0=sz[:], scalar1=-1.0 / V, scalar2=None, op0=ALU.mult)
+            T[("z", e)] = z
+            T[("nm", e)] = nm
+
+        def ln_squares(e):
+            ssq = stp.tile([P, BC], F32, name="ssq")
+            for bc in range(BC):
+                junk = lnp.tile([P, V], F32, name="junk")
+                nc.scalar.activation(
+                    out=junk[:],
+                    in_=T[("z", e)][:, bc, :],
+                    func=ACT.Square,
+                    bias=T[("nm", e)][:, bc : bc + 1],
+                    scale=1.0,
+                    accum_out=ssq[:, bc : bc + 1],
+                )
+            T[("ssq", e)] = ssq
+
+        def ln_gain(e):
+            tt = lnp.tile([P, BC, V], F32, name="tt")
+            for bc in range(BC):
+                nc.vector.scalar_tensor_tensor(
+                    out=tt[:, bc, :],
+                    in0=T[("z", e)][:, bc, :],
+                    scalar=T[("nm", e)][:, bc : bc + 1],
+                    in1=gbc[:, e * V : (e + 1) * V],
+                    op0=ALU.add,
+                    op1=ALU.mult,
+                )
+            T[("tt", e)] = tt
+
+        def ln_var(e):
+            ve = stp.tile([P, BC], F32, name="ve")
+            nc.vector.tensor_scalar(
+                out=ve[:], in0=T[("ssq", e)][:], scalar1=1.0 / V, scalar2=LN_EPS, op0=ALU.mult, op1=ALU.add
+            )
+            rstd = stp.tile([P, BC], F32, name="rstd")
+            nc.gpsimd.tensor_tensor(out=rstd[:], in0=ve[:], in1=negh[:], op=ALU.pow)
+            T[("rstd", e)] = rstd
+
+        def ln_out(e):
+            o = lnp.tile([P, BC, V], F32, name="o")
+            for bc in range(BC):
+                nc.vector.scalar_tensor_tensor(
+                    out=o[:, bc, :],
+                    in0=T[("tt", e)][:, bc, :],
+                    scalar=T[("rstd", e)][:, bc : bc + 1],
+                    in1=bbc[:, e * V : (e + 1) * V],
+                    op0=ALU.mult,
+                    op1=ALU.add,
+                )
+            nc.sync.dma_start(out=out_v[:, :, e, :], in_=o[:])
+
+        cv_v = causal_vars.rearrange("(c p) j v -> p c (j v)", p=P)
         cvr = const.tile([P, BC, K], BF16, name="cvr")
-        nc.sync.dma_start(out=cvr[:], in_=causal_vars.rearrange("(c p) j v -> p c (j v)", p=P))
         adjb = const.tile([P, D * D], BF16, name="adjb")
-        nc.sync.dma_start(out=adjb[:], in_=adj_soft.rearrange("i j -> (i j)").partition_broadcast(P))
         b1t = const.tile([P, P], BF16, name="b1t")
-        nc.vector.memset(b1t[:], 0.0)
-        nc.sync.dma_start(out=b1t[0 : D * C, :], in_=b1.rearrange("i (c m) -> (i c) m", m=P))
-        for g in range(1, G):
-            load_w1(0, g)
         w2r = const.tile([P, D, PACK, V], BF16, name="w2r")
-        nc.sync.dma_start(out=w2r[:, 0:4], in_=W2[0:4].rearrange("i (t p) v -> p i t v", p=P))
-        for g in range(G):
-            load_w1(1, g)
         b2bc = const.tile([P, D * V], BF16, name="b2bc")
-        nc.sync.dma_start(out=b2bc[:], in_=b2.rearrange("i v -> (i v)").partition_broadcast(P))
         gbc = const.tile([P, D * V], BF16, name="gbc")
-        nc.sync.dma_start(out=gbc[:], in_=gamma.rearrange("i v -> (i v)").partition_broadcast(P))
         bbc = const.tile([P, D * V], BF16, name="bbc")
-        nc.sync.dma_start(out=bbc[:], in_=beta.rearrange("i v -> (i v)").partition_broadcast(P))
-        for q in range(1, 4):
+        nc.vector.memset(b1t[:], 0.0)
+
+        def load_w2(q):
             nc.sync.dma_start(
                 out=w2r[:, 4 * q : 4 * q + 4],
                 in_=W2[4 * q : 4 * q + 4].rearrange("i (t p) v -> p i t v", p=P),
             )
+
+        load_w1(0, 0)
+        load_w1(0, 1)
+        load_w1(0, 2)
+        nc.sync.dma_start(out=cvr[:, 0, :], in_=cv_v[:, 0, :])
+        load_w1(0, 3)
+        nc.sync.dma_start(out=cvr[:, 1, :], in_=cv_v[:, 1, :])
+        nc.sync.dma_start(out=adjb[:], in_=adj_soft.rearrange("i j -> (i j)").partition_broadcast(P))
+        nc.sync.dma_start(out=b1t[0 : D * C, :], in_=b1.rearrange("i (c m) -> (i c) m", m=P))
+        load_w1(1, 0)
+        load_w1(1, 1)
+        load_w2(0)
+        load_w1(1, 2)
+        load_w1(1, 3)
+        nc.sync.dma_start(out=b2bc[:], in_=b2.rearrange("i v -> (i v)").partition_broadcast(P))
+        nc.sync.dma_start(out=gbc[:], in_=gamma.rearrange("i v -> (i v)").partition_broadcast(P))
+        nc.sync.dma_start(out=bbc[:], in_=beta.rearrange("i v -> (i v)").partition_broadcast(P))
 
         ident_f = const.tile([P, P], F32, name="ident_f")
         make_identity(nc, ident_f[:])
@@ -93,170 +276,98 @@ def tile_structuralequationmodels_kernel(
         make_identity(nc, ident_b[:])
         negh = const.tile([P, BC], F32, name="negh")
         nc.vector.memset(negh[:], -0.5)
-
+        warm = const.tile([P, 1], F32, name="warm")
+        nc.scalar.activation(out=warm[:], in_=negh[:, 0:1], func=ACT.Gelu)
         adjcol = const.tile([P, D * G], F32, name="adjcol")
-        for q in range(4):
-            rows = slice(32 * q, 32 * q + 32)
-            nc.vector.tensor_copy(
-                out=adjcol[rows, :].rearrange("p (i g) -> p i g", g=G),
-                in_=adjb[rows, :].rearrange("p (i g q) -> p i g q", g=G, q=4)[:, :, :, q],
-            )
-
-        b1ps = ps_set.tile([P, P], BF16, name="b1ps", tag="set")
-        nc.tensor.transpose(b1ps[:], b1t[:], ident_b[:])
         b1col = const.tile([P, D * C], F32, name="b1col")
-        nc.vector.tensor_copy(out=b1col[:], in_=b1ps[:, 0 : D * C])
-
         cvg = const.tile([P, G, B, PACK], BF16, name="cvg", align_bytes=64)
-        cvw = cvr[:].bitcast(F32)
-        cvgw = cvg[:].bitcast(F32)
-        for g in range(G):
-            xt = ps_set.tile([P, 2, B], F32, name="xt", tag="set")
-            for u in range(2):
+
+        def setup():
+            cvw = cvr[:].bitcast(F32)
+            cvgw = cvg[:].bitcast(F32)
+            for g in range(G):
+                xt = ps_set.tile([P, 2, B], F32, name="xt", tag="set")
                 for bc in range(BC):
-                    nc.tensor.transpose(
-                        xt[:, u, bc * P : (bc + 1) * P],
-                        cvw[:, bc, 256 * g + u : 256 * (g + 1) : 2],
-                        ident_f[:],
-                    )
-            nc.vector.tensor_copy(out=cvgw[:, g], in_=xt[:].rearrange("p u b -> p b u"))
-
-        out_v = out.rearrange("(c p) i v -> p c i v", p=P)
-
-        for i in range(D):
-            if i + AHEAD < D:
-                for g in range(G):
-                    load_w1(i + AHEAD, g)
-
-            xs = xp.tile([P, G, B * PACK], BF16, name="xs", align_bytes=64)
-            for g in range(G):
-                nc.vector.tensor_scalar(
-                    out=xs[:, g, :],
-                    in0=cvg[:, g].rearrange("p b t -> p (b t)"),
-                    scalar1=adjcol[:, G * i + g : G * i + g + 1],
-                    scalar2=None,
-                    op0=ALU.mult,
-                )
-            xc = xqp.tile([P, G * B], U32, name="xc", align_bytes=64)
-            xsc = xqp.tile([P, G * B], U8, name="xsc", align_bytes=64)
-            nc.vector.quantize_mx(
-                out=xc[:].bitcast(FP8X4), scales=xsc[:], in_=xs[:].rearrange("p g e -> p (g e)")
-            )
-
-            w1c = w1qp.tile([P, G, H], U32, name="w1c", align_bytes=64)
-            w1s = w1qp.tile([P, G, H], U8, name="w1s", align_bytes=64)
-            for g in range(G):
-                grp = grpp.tile([P, H, PACK], BF16, name="grp", align_bytes=64)
-                copy = nc.scalar.copy if g in SCALAR_UNITS else nc.vector.tensor_copy
-                regroup(copy, grp[:], raws[(i, g)][:].rearrange("p (t h) -> p t h", t=PACK))
-                nc.vector.quantize_mx(
-                    out=w1c[:, g, :].bitcast(FP8X4),
-                    scales=w1s[:, g, :],
-                    in_=grp[:].rearrange("p w t -> p (w t)"),
-                )
-
-            g2 = hp.tile([P, V, PACK], BF16, name="g2", align_bytes=64)
-            regroup(nc.vector.tensor_copy, g2[:], w2r[:, i])
-            w2c = hp.tile([P, V], U32, name="w2c", align_bytes=64)
-            w2s = hp.tile([P, V], U8, name="w2s", align_bytes=64)
-            nc.vector.quantize_mx(
-                out=w2c[:].bitcast(FP8X4), scales=w2s[:], in_=g2[:].rearrange("p w t -> p (w t)")
-            )
-
-            ht = hp.tile([P, C, B], BF16, name="ht")
-            for cp in range(C // 2):
-                hps = ps_h.tile([P, 2, B], F32, name="hps")
-                for cc in range(2):
-                    c = 2 * cp + cc
-                    for g in range(G):
-                        nc.tensor.matmul_mx(
-                            out=hps[:, cc, :],
-                            lhsT=w1c[:, g, c * P : (c + 1) * P].bitcast(FP8X4),
-                            lhsT_scale=w1s[:, g, c * P : (c + 1) * P],
-                            rhs=xc[:, g * B : (g + 1) * B].bitcast(FP8X4),
-                            rhs_scale=xsc[:, g * B : (g + 1) * B],
-                            start=(g == 0),
-                            stop=(g == G - 1),
+                    for u in range(2):
+                        nc.tensor.transpose(
+                            xt[:, u, bc * P : (bc + 1) * P],
+                            cvw[:, bc, 256 * g + u : 256 * (g + 1) : 2],
+                            ident_f[:],
                         )
-                for cc in range(2):
-                    c = 2 * cp + cc
-                    nc.scalar.activation(
-                        out=ht[:, c, :],
-                        in_=hps[:, cc, :],
-                        func=ACT.Gelu,
-                        bias=b1col[:, C * i + c : C * i + c + 1],
-                        scale=1.0,
-                    )
-            hg = hp.tile([P, B, PACK], BF16, name="hg", align_bytes=64)
-            regroup(nc.vector.tensor_copy, hg[:], ht[:])
-            hc = hp.tile([P, B], U32, name="hc", align_bytes=64)
-            hs = hp.tile([P, B], U8, name="hs", align_bytes=64)
-            nc.vector.quantize_mx(
-                out=hc[:].bitcast(FP8X4), scales=hs[:], in_=hg[:].rearrange("p w t -> p (w t)")
-            )
+                nc.vector.tensor_copy(out=cvgw[:, g], in_=xt[:].rearrange("p u b -> p b u"))
+            for q in range(4):
+                rows = slice(32 * q, 32 * q + 32)
+                nc.vector.tensor_copy(
+                    out=adjcol[rows, :].rearrange("p (i g) -> p i g", g=G),
+                    in_=adjb[rows, :].rearrange("p (i g q) -> p i g q", g=G, q=4)[:, :, :, q],
+                )
+            b1ps = ps_set.tile([P, P], BF16, name="b1ps", tag="set")
+            nc.tensor.transpose(b1ps[:], b1t[:], ident_b[:])
+            nc.vector.tensor_copy(out=b1col[:], in_=b1ps[:, 0 : D * C])
 
-            yps = ps_y.tile([P, BC, V], F32, name="yps")
-            for bc in range(BC):
-                nc.tensor.matmul_mx(
-                    out=yps[:, bc, :],
-                    lhsT=hc[:, bc * P : (bc + 1) * P].bitcast(FP8X4),
-                    lhsT_scale=hs[:, bc * P : (bc + 1) * P],
-                    rhs=w2c[:].bitcast(FP8X4),
-                    rhs_scale=w2s[:],
-                    start=True,
-                    stop=True,
-                )
+        def live(e):
+            return 0 <= e < D
 
-            cols = slice(i * V, (i + 1) * V)
-            z = lnp.tile([P, BC, V], F32, name="z")
-            sz = stp.tile([P, BC], F32, name="sz")
-            for bc in range(BC):
-                nc.vector.scalar_tensor_tensor(
-                    out=z[:, bc, :],
-                    in0=yps[:, bc, :],
-                    scalar=1.0,
-                    in1=b2bc[:, cols],
-                    op0=ALU.mult,
-                    op1=ALU.add,
-                    accum_out=sz[:, bc : bc + 1],
-                )
-            nm = stp.tile([P, BC], F32, name="nm")
-            nc.vector.tensor_scalar(out=nm[:], in0=sz[:], scalar1=-1.0 / V, scalar2=None, op0=ALU.mult)
-            ssq = stp.tile([P, BC], F32, name="ssq")
-            for bc in range(BC):
-                junk = lnp.tile([P, V], F32, name="junk")
-                nc.scalar.activation(
-                    out=junk[:],
-                    in_=z[:, bc, :],
-                    func=ACT.Square,
-                    bias=nm[:, bc : bc + 1],
-                    scale=1.0,
-                    accum_out=ssq[:, bc : bc + 1],
-                )
-            ve = stp.tile([P, BC], F32, name="ve")
-            nc.gpsimd.tensor_scalar(
-                out=ve[:], in0=ssq[:], scalar1=1.0 / V, scalar2=LN_EPS, op0=ALU.mult, op1=ALU.add
-            )
-            rstd = stp.tile([P, BC], F32, name="rstd")
-            nc.gpsimd.tensor_tensor(out=rstd[:], in0=ve[:], in1=negh[:], op=ALU.pow)
-            tt = lnp.tile([P, BC, V], F32, name="tt")
-            o = lnp.tile([P, BC, V], F32, name="o")
-            for bc in range(BC):
-                nc.vector.scalar_tensor_tensor(
-                    out=tt[:, bc, :],
-                    in0=z[:, bc, :],
-                    scalar=nm[:, bc : bc + 1],
-                    in1=gbc[:, cols],
-                    op0=ALU.add,
-                    op1=ALU.mult,
-                )
-            for bc in range(BC):
-                nc.vector.scalar_tensor_tensor(
-                    out=o[:, bc, :],
-                    in0=tt[:, bc, :],
-                    scalar=rstd[:, bc : bc + 1],
-                    in1=bbc[:, cols],
-                    op0=ALU.mult,
-                    op1=ALU.add,
-                )
-            nc.sync.dma_start(out=out_v[:, :, i, :], in_=o[:])
+        for r in range(D + 2):
+            e0, e1, e2 = r, r - 1, r - 2
+            if live(e0 + AHEAD):
+                for g in range(G):
+                    load_w1(e0 + AHEAD, g)
+                if 1 <= e0 <= 3:
+                    load_w2(e0)
+            if live(e1):
+                w1_quant(e1, UC)
+                mm1(e1, UC)
+            if e0 == 0:
+                w1_regroup(e0, UA, nc.scalar.copy)
+                w1_regroup(e0, UV, nc.vector.tensor_copy)
+                w1_regroup(e0, UB, nc.scalar.copy)
+                w1_quant(e0, UA)
+                w1_quant(e0, UV)
+                w1_quant(e0, UB)
+                w1_regroup(e0, UC, nc.scalar.copy)
+                setup()
+                x_scale(e0)
+                w2_regroup(e0)
+                x_quant(e0)
+                mm1(e0, UA)
+                mm1(e0, UB)
+                mm1(e0, UV)
+                w2_quant(e0)
+                continue
+            if live(e0):
+                w1_regroup(e0, UA, nc.scalar.copy)
+                x_scale(e0)
+            if live(e2):
+                ln_mean(e2)
+            if live(e0):
+                w1_regroup(e0, UB, nc.scalar.copy)
+            if live(e2):
+                ln_squares(e2)
+            if live(e1):
+                gelu(e1)
+            if live(e0):
+                w1_quant(e0, UA)
+                x_quant(e0)
+                mm1(e0, UA)
+                w1_regroup(e0, UV, nc.vector.tensor_copy)
+                w1_quant(e0, UB)
+                mm1(e0, UB)
+            if live(e2):
+                ln_gain(e2)
+                ln_var(e2)
+            if live(e0):
+                w1_regroup(e0, UC, nc.scalar.copy)
+                w1_quant(e0, UV)
+                mm1(e0, UV)
+            if live(e1):
+                h_regroup(e1)
+            if live(e0):
+                w2_regroup(e0)
+            if live(e2):
+                ln_out(e2)
+            if live(e1):
+                h_quant(e1)
+                mm2(e1)
+            if live(e0):
+                w2_quant(e0)

@@ -46,8 +46,8 @@ def tile_structuralequationmodels_kernel(
         xp = ctx.enter_context(tc.tile_pool(name="xp", bufs=2))
         xqp = ctx.enter_context(tc.tile_pool(name="xqp", bufs=3))
         hp = ctx.enter_context(tc.tile_pool(name="hp", bufs=3))
-        lnp = ctx.enter_context(tc.tile_pool(name="lnp", bufs=3))
-        stp = ctx.enter_context(tc.tile_pool(name="stp", bufs=4))
+        lnp = ctx.enter_context(tc.tile_pool(name="lnp", bufs=4))
+        stp = ctx.enter_context(tc.tile_pool(name="stp", bufs=5))
         ps_set = ctx.enter_context(tc.psum_pool(name="ps_set", bufs=2))
         ps_h = ctx.enter_context(tc.psum_pool(name="ps_h", bufs=1))
         ps_y = ctx.enter_context(tc.psum_pool(name="ps_y", bufs=2))
@@ -308,8 +308,8 @@ def tile_structuralequationmodels_kernel(
         def live(e):
             return 0 <= e < D
 
-        for r in range(D + 2):
-            e0, e1, e2 = r, r - 1, r - 2
+        for r in range(D + 4):
+            e0, e1, e2, e3, e4 = r, r - 1, r - 2, r - 3, r - 4
             if live(e0 + AHEAD):
                 for g in range(G):
                     load_w1(e0 + AHEAD, g)
@@ -338,6 +338,8 @@ def tile_structuralequationmodels_kernel(
             if live(e0):
                 w1_regroup(e0, UA, nc.scalar.copy)
                 x_scale(e0)
+            if live(e3):
+                ln_var(e3)
             if live(e2):
                 ln_mean(e2)
             if live(e0):
@@ -355,7 +357,6 @@ def tile_structuralequationmodels_kernel(
                 mm1(e0, UB)
             if live(e2):
                 ln_gain(e2)
-                ln_var(e2)
             if live(e0):
                 w1_regroup(e0, UC, nc.scalar.copy)
                 w1_quant(e0, UV)
@@ -364,8 +365,8 @@ def tile_structuralequationmodels_kernel(
                 h_regroup(e1)
             if live(e0):
                 w2_regroup(e0)
-            if live(e2):
-                ln_out(e2)
+            if live(e4):
+                ln_out(e4)
             if live(e1):
                 h_quant(e1)
                 mm2(e1)

@@ -25,6 +25,9 @@ FLOPS = 2 * B * D * (K * H + H * V)
 AHEAD = 2
 UA, UV, UB, UC = 0, 1, 2, 3
 PASS_ORDER = (UA, UB, UV, UC)
+POW_GROUP = 4
+OUT_LAG = 7
+SV_COLS = 64
 
 
 def regroup(copy, dst, src):
@@ -64,10 +67,11 @@ def tile_structuralequationmodels_kernel(
             )
             T[("raw", e, g)] = raw
 
-        def w1_regroup(e, g, copy):
-            grp = grpp.tile([P, H, PACK], BF16, name="grp", align_bytes=64)
-            regroup(copy, grp[:], T[("raw", e, g)][:].rearrange("p (t h) -> p t h", t=PACK))
-            T[("grp", e, g)] = grp
+        def w1_regroup(e, g, copy, lo=0, hi=H):
+            if ("grp", e, g) not in T:
+                T[("grp", e, g)] = grpp.tile([P, H, PACK], BF16, name="grp", align_bytes=64)
+            raw3 = T[("raw", e, g)][:].rearrange("p (t h) -> p t h", t=PACK)
+            regroup(copy, T[("grp", e, g)][:, lo:hi, :], raw3[:, :, lo:hi])
 
         def w1_quant(e, g):
             if g == PASS_ORDER[0]:
@@ -183,9 +187,14 @@ def tile_structuralequationmodels_kernel(
                     op1=ALU.add,
                     accum_out=sz[:, bc : bc + 1],
                 )
-            nm = stp.tile([P, BC], F32, name="nm")
-            nc.vector.tensor_scalar(out=nm[:], in0=sz[:], scalar1=-1.0 / V, scalar2=None, op0=ALU.mult)
             T[("z", e)] = z
+            T[("sz", e)] = sz
+
+        def ln_negmean(e):
+            nm = stp.tile([P, BC], F32, name="nm")
+            nc.vector.tensor_scalar(
+                out=nm[:], in0=T[("sz", e)][:], scalar1=-1.0 / V, scalar2=None, op0=ALU.mult
+            )
             T[("nm", e)] = nm
 
         def ln_squares(e):
@@ -203,7 +212,7 @@ def tile_structuralequationmodels_kernel(
             T[("ssq", e)] = ssq
 
         def ln_gain(e):
-            tt = lnp.tile([P, BC, V], F32, name="tt")
+            tt = lnp.tile([P, BC, V], F32, name="tt", bufs=OUT_LAG)
             for bc in range(BC):
                 nc.vector.scalar_tensor_tensor(
                     out=tt[:, bc, :],
@@ -215,14 +224,26 @@ def tile_structuralequationmodels_kernel(
                 )
             T[("tt", e)] = tt
 
-        def ln_var(e):
-            ve = stp.tile([P, BC], F32, name="ve")
+        def ln_var(e, group):
+            first, last = group
+            width = (last - first + 1) * BC
+            if e == first:
+                T[("ve", first)] = stp.tile([P, width], F32, name="ve")
+            ve = T[("ve", first)]
+            at = (e - first) * BC
             nc.vector.tensor_scalar(
-                out=ve[:], in0=T[("ssq", e)][:], scalar1=1.0 / V, scalar2=LN_EPS, op0=ALU.mult, op1=ALU.add
+                out=ve[:, at : at + BC],
+                in0=T[("ssq", e)][:],
+                scalar1=1.0 / V,
+                scalar2=LN_EPS,
+                op0=ALU.mult,
+                op1=ALU.add,
             )
-            rstd = stp.tile([P, BC], F32, name="rstd")
-            nc.gpsimd.tensor_tensor(out=rstd[:], in0=ve[:], in1=negh[:], op=ALU.pow)
-            T[("rstd", e)] = rstd
+            if e == last:
+                rstd = stp.tile([P, width], F32, name="rstd")
+                nc.gpsimd.tensor_tensor(out=rstd[:], in0=ve[:], in1=negh[:, 0:width], op=ALU.pow)
+                for m in range(first, last + 1):
+                    T[("rstd", m)] = rstd[:, (m - first) * BC : (m - first + 1) * BC]
 
         def ln_out(e):
             o = lnp.tile([P, BC, V], F32, name="o")
@@ -274,7 +295,7 @@ def tile_structuralequationmodels_kernel(
         make_identity(nc, ident_f[:])
         ident_b = const.tile([P, P], BF16, name="ident_b")
         make_identity(nc, ident_b[:])
-        negh = const.tile([P, BC], F32, name="negh")
+        negh = const.tile([P, POW_GROUP * BC], F32, name="negh")
         nc.vector.memset(negh[:], -0.5)
         warm = const.tile([P, 1], F32, name="warm")
         nc.scalar.activation(out=warm[:], in_=negh[:, 0:1], func=ACT.Gelu)
@@ -305,11 +326,18 @@ def tile_structuralequationmodels_kernel(
             nc.tensor.transpose(b1ps[:], b1t[:], ident_b[:])
             nc.vector.tensor_copy(out=b1col[:], in_=b1ps[:, 0 : D * C])
 
+        def pow_group(e):
+            if e < D - 4:
+                return (e - e % POW_GROUP, e - e % POW_GROUP + POW_GROUP - 1)
+            if e < D - 2:
+                return (D - 4, D - 3)
+            return (e, e)
+
         def live(e):
             return 0 <= e < D
 
-        for r in range(D + 4):
-            e0, e1, e2, e3, e4 = r, r - 1, r - 2, r - 3, r - 4
+        for r in range(D):
+            e0, e1, e2, e3, e4 = r, r - 1, r - 2, r - 3, r - OUT_LAG
             if live(e0 + AHEAD):
                 for g in range(G):
                     load_w1(e0 + AHEAD, g)
@@ -318,6 +346,9 @@ def tile_structuralequationmodels_kernel(
             if live(e1):
                 w1_quant(e1, UC)
                 mm1(e1, UC)
+            if live(e2):
+                h_quant(e2)
+                mm2(e2)
             if e0 == 0:
                 w1_regroup(e0, UA, nc.scalar.copy)
                 w1_regroup(e0, UV, nc.vector.tensor_copy)
@@ -339,36 +370,62 @@ def tile_structuralequationmodels_kernel(
                 w1_regroup(e0, UA, nc.scalar.copy)
                 x_scale(e0)
             if live(e3):
-                ln_var(e3)
+                ln_var(e3, pow_group(e3))
             if live(e2):
                 ln_mean(e2)
             if live(e0):
                 w1_regroup(e0, UB, nc.scalar.copy)
-            if live(e2):
-                ln_squares(e2)
             if live(e1):
                 gelu(e1)
             if live(e0):
                 w1_quant(e0, UA)
+            if live(e2):
+                ln_negmean(e2)
+            if live(e0):
                 x_quant(e0)
                 mm1(e0, UA)
-                w1_regroup(e0, UV, nc.vector.tensor_copy)
+                w1_regroup(e0, UV, nc.scalar.copy, 0, SV_COLS)
+                w1_regroup(e0, UV, nc.vector.tensor_copy, SV_COLS, H)
+                w1_regroup(e0, UC, nc.scalar.copy)
                 w1_quant(e0, UB)
                 mm1(e0, UB)
             if live(e2):
+                ln_squares(e2)
                 ln_gain(e2)
+            if live(e4):
+                ln_out(e4)
             if live(e0):
-                w1_regroup(e0, UC, nc.scalar.copy)
-                w1_quant(e0, UV)
-                mm1(e0, UV)
+                w2_regroup(e0)
             if live(e1):
                 h_regroup(e1)
             if live(e0):
-                w2_regroup(e0)
-            if live(e4):
-                ln_out(e4)
-            if live(e1):
-                h_quant(e1)
-                mm2(e1)
-            if live(e0):
+                w1_quant(e0, UV)
+                mm1(e0, UV)
                 w2_quant(e0)
+
+        w1_quant(D - 1, UC)
+        mm1(D - 1, UC)
+        h_quant(D - 2)
+        mm2(D - 2)
+        ln_var(D - 3, pow_group(D - 3))
+        gelu(D - 1)
+        ln_out(D - 7)
+        ln_mean(D - 2)
+        ln_out(D - 6)
+        ln_negmean(D - 2)
+        ln_squares(D - 2)
+        ln_gain(D - 2)
+        ln_out(D - 5)
+        h_regroup(D - 1)
+        ln_var(D - 2, pow_group(D - 2))
+        ln_out(D - 4)
+        h_quant(D - 1)
+        mm2(D - 1)
+        ln_out(D - 3)
+        ln_mean(D - 1)
+        ln_negmean(D - 1)
+        ln_squares(D - 1)
+        ln_gain(D - 1)
+        ln_out(D - 2)
+        ln_var(D - 1, pow_group(D - 1))
+        ln_out(D - 1)

@@ -27,7 +27,8 @@ UA, UV, UB, UC = 0, 1, 2, 3
 PASS_ORDER = (UA, UB, UV, UC)
 POW_GROUP = 4
 OUT_LAG = 7
-SV_COLS = 64
+SV_COLS = 0
+VC_COLS = 64
 
 
 def regroup(copy, dst, src):
@@ -384,9 +385,12 @@ def tile_structuralequationmodels_kernel(
             if live(e0):
                 x_quant(e0)
                 mm1(e0, UA)
-                w1_regroup(e0, UV, nc.scalar.copy, 0, SV_COLS)
+                if SV_COLS > 0:
+                    w1_regroup(e0, UV, nc.scalar.copy, 0, SV_COLS)
                 w1_regroup(e0, UV, nc.vector.tensor_copy, SV_COLS, H)
-                w1_regroup(e0, UC, nc.scalar.copy)
+                w1_regroup(e0, UC, nc.scalar.copy, 0, H - VC_COLS)
+                if VC_COLS > 0:
+                    w1_regroup(e0, UC, nc.vector.tensor_copy, H - VC_COLS, H)
                 w1_quant(e0, UB)
                 mm1(e0, UB)
             if live(e2):

@@ -27,8 +27,14 @@ UA, UV, UB, UC = 0, 1, 2, 3
 PASS_ORDER = (UA, UB, UV, UC)
 POW_GROUP = 4
 OUT_LAG = 7
-SV_COLS = 0
-VC_COLS = 64
+
+
+def split(r):
+    if r <= 2:
+        return ((320, 192)[r - 1], 0)
+    if r < OUT_LAG:
+        return (0, 160)
+    return (48, 0)
 
 
 def regroup(copy, dst, src):
@@ -36,6 +42,18 @@ def regroup(copy, dst, src):
         out=dst.rearrange("p (c i) t -> p c t i", i=4),
         in_=src.rearrange("p t (c i) -> p c t i", i=4),
     )
+
+
+def pow_group(e):
+    if e < D - 4:
+        return (e - e % POW_GROUP, e - e % POW_GROUP + POW_GROUP - 1)
+    if e < D - 2:
+        return (D - 4, D - 3)
+    return (e, e)
+
+
+def live(e):
+    return 0 <= e < D
 
 
 def tile_structuralequationmodels_kernel(
@@ -50,8 +68,8 @@ def tile_structuralequationmodels_kernel(
         xp = ctx.enter_context(tc.tile_pool(name="xp", bufs=2))
         xqp = ctx.enter_context(tc.tile_pool(name="xqp", bufs=3))
         hp = ctx.enter_context(tc.tile_pool(name="hp", bufs=3))
-        lnp = ctx.enter_context(tc.tile_pool(name="lnp", bufs=4))
-        stp = ctx.enter_context(tc.tile_pool(name="stp", bufs=5))
+        lnp = ctx.enter_context(tc.tile_pool(name="lnp", bufs=3))
+        stp = ctx.enter_context(tc.tile_pool(name="stp", bufs=3))
         ps_set = ctx.enter_context(tc.psum_pool(name="ps_set", bufs=2))
         ps_h = ctx.enter_context(tc.psum_pool(name="ps_h", bufs=1))
         ps_y = ctx.enter_context(tc.psum_pool(name="ps_y", bufs=2))
@@ -60,19 +78,22 @@ def tile_structuralequationmodels_kernel(
         T = {}
         out_v = out.rearrange("(c p) i v -> p c i v", p=P)
 
-        def load_w1(e, g):
-            raw = rawp.tile([P, PACK * H], BF16, name="raw")
-            nc.sync.dma_start(
-                out=raw[:],
-                in_=W1[e][g * K_PASS : (g + 1) * K_PASS, :].rearrange("(p t) h -> p (t h)", t=PACK),
-            )
+        def load_w1(e, g, pieces=1):
+            raw = rawp.tile([P, PACK, H], BF16, name="raw")
+            rows = W1[e][g * K_PASS : (g + 1) * K_PASS, :].rearrange("(p t) h -> p t h", t=PACK)
+            width = H // pieces
+            for n in range(pieces):
+                nc.sync.dma_start(
+                    out=raw[:, :, n * width : (n + 1) * width], in_=rows[:, :, n * width : (n + 1) * width]
+                )
             T[("raw", e, g)] = raw
 
         def w1_regroup(e, g, copy, lo=0, hi=H):
+            if hi <= lo:
+                return
             if ("grp", e, g) not in T:
                 T[("grp", e, g)] = grpp.tile([P, H, PACK], BF16, name="grp", align_bytes=64)
-            raw3 = T[("raw", e, g)][:].rearrange("p (t h) -> p t h", t=PACK)
-            regroup(copy, T[("grp", e, g)][:, lo:hi, :], raw3[:, :, lo:hi])
+            regroup(copy, T[("grp", e, g)][:, lo:hi, :], T[("raw", e, g)][:, :, lo:hi])
 
         def w1_quant(e, g):
             if g == PASS_ORDER[0]:
@@ -175,8 +196,8 @@ def tile_structuralequationmodels_kernel(
                 )
             T[("yps", e)] = yps
 
-        def ln_mean(e):
-            z = lnp.tile([P, BC, V], F32, name="z")
+        def ln_sum(e):
+            z = lnp.tile([P, BC, V], F32, name="z", bufs=OUT_LAG)
             sz = stp.tile([P, BC], F32, name="sz")
             for bc in range(BC):
                 nc.vector.scalar_tensor_tensor(
@@ -192,28 +213,42 @@ def tile_structuralequationmodels_kernel(
             T[("sz", e)] = sz
 
         def ln_negmean(e):
-            nm = stp.tile([P, BC], F32, name="nm")
+            nm = stp.tile([P, BC], F32, name="nm", bufs=OUT_LAG)
             nc.vector.tensor_scalar(
                 out=nm[:], in0=T[("sz", e)][:], scalar1=-1.0 / V, scalar2=None, op0=ALU.mult
             )
             T[("nm", e)] = nm
 
         def ln_squares(e):
-            ssq = stp.tile([P, BC], F32, name="ssq")
+            first, last = pow_group(e)
+            if e == first:
+                T[("ssq", first)] = stp.tile([P, (last - first + 1) * BC], F32, name="ssq")
             for bc in range(BC):
                 junk = lnp.tile([P, V], F32, name="junk")
+                at = (e - first) * BC + bc
                 nc.scalar.activation(
                     out=junk[:],
                     in_=T[("z", e)][:, bc, :],
                     func=ACT.Square,
                     bias=T[("nm", e)][:, bc : bc + 1],
                     scale=1.0,
-                    accum_out=ssq[:, bc : bc + 1],
+                    accum_out=T[("ssq", first)][:, at : at + 1],
                 )
-            T[("ssq", e)] = ssq
+
+        def ln_rstd(e):
+            first, last = pow_group(e)
+            width = (last - first + 1) * BC
+            ve = stp.tile([P, width], F32, name="ve")
+            nc.vector.tensor_scalar(
+                out=ve[:], in0=T[("ssq", first)][:], scalar1=1.0 / V, scalar2=LN_EPS, op0=ALU.mult, op1=ALU.add
+            )
+            rstd = stp.tile([P, width], F32, name="rstd")
+            nc.gpsimd.tensor_tensor(out=rstd[:], in0=ve[:], in1=negh[:, 0:width], op=ALU.pow)
+            for m in range(first, last + 1):
+                T[("rstd", m)] = rstd[:, (m - first) * BC : (m - first + 1) * BC]
 
         def ln_gain(e):
-            tt = lnp.tile([P, BC, V], F32, name="tt", bufs=OUT_LAG)
+            tt = lnp.tile([P, BC, V], F32, name="tt")
             for bc in range(BC):
                 nc.vector.scalar_tensor_tensor(
                     out=tt[:, bc, :],
@@ -224,27 +259,6 @@ def tile_structuralequationmodels_kernel(
                     op1=ALU.mult,
                 )
             T[("tt", e)] = tt
-
-        def ln_var(e, group):
-            first, last = group
-            width = (last - first + 1) * BC
-            if e == first:
-                T[("ve", first)] = stp.tile([P, width], F32, name="ve")
-            ve = T[("ve", first)]
-            at = (e - first) * BC
-            nc.vector.tensor_scalar(
-                out=ve[:, at : at + BC],
-                in0=T[("ssq", e)][:],
-                scalar1=1.0 / V,
-                scalar2=LN_EPS,
-                op0=ALU.mult,
-                op1=ALU.add,
-            )
-            if e == last:
-                rstd = stp.tile([P, width], F32, name="rstd")
-                nc.gpsimd.tensor_tensor(out=rstd[:], in0=ve[:], in1=negh[:, 0:width], op=ALU.pow)
-                for m in range(first, last + 1):
-                    T[("rstd", m)] = rstd[:, (m - first) * BC : (m - first + 1) * BC]
 
         def ln_out(e):
             o = lnp.tile([P, BC, V], F32, name="o")
@@ -275,7 +289,7 @@ def tile_structuralequationmodels_kernel(
                 in_=W2[4 * q : 4 * q + 4].rearrange("i (t p) v -> p i t v", p=P),
             )
 
-        load_w1(0, 0)
+        load_w1(0, 0, pieces=2)
         load_w1(0, 1)
         load_w1(0, 2)
         nc.sync.dma_start(out=cvr[:, 0, :], in_=cv_v[:, 0, :])
@@ -285,8 +299,8 @@ def tile_structuralequationmodels_kernel(
         nc.sync.dma_start(out=b1t[0 : D * C, :], in_=b1.rearrange("i (c m) -> (i c) m", m=P))
         load_w1(1, 0)
         load_w1(1, 1)
-        load_w2(0)
         load_w1(1, 2)
+        load_w2(0)
         load_w1(1, 3)
         nc.sync.dma_start(out=b2bc[:], in_=b2.rearrange("i v -> (i v)").partition_broadcast(P))
         nc.sync.dma_start(out=gbc[:], in_=gamma.rearrange("i v -> (i v)").partition_broadcast(P))
@@ -327,109 +341,107 @@ def tile_structuralequationmodels_kernel(
             nc.tensor.transpose(b1ps[:], b1t[:], ident_b[:])
             nc.vector.tensor_copy(out=b1col[:], in_=b1ps[:, 0 : D * C])
 
-        def pow_group(e):
-            if e < D - 4:
-                return (e - e % POW_GROUP, e - e % POW_GROUP + POW_GROUP - 1)
-            if e < D - 2:
-                return (D - 4, D - 3)
-            return (e, e)
+        s_copy = nc.scalar.copy
+        v_copy = nc.vector.tensor_copy
 
-        def live(e):
-            return 0 <= e < D
+        for g in range(G):
+            load_w1(AHEAD, g)
+        w1_regroup(0, UA, s_copy, 0, H // 2)
+        w1_regroup(0, UA, s_copy, H // 2, H)
+        w1_regroup(0, UV, v_copy)
+        w1_regroup(0, UB, s_copy)
+        w1_quant(0, UA)
+        w1_quant(0, UV)
+        w1_quant(0, UB)
+        w1_regroup(0, UC, s_copy)
+        setup()
+        x_scale(0)
+        w2_regroup(0)
+        x_quant(0)
+        mm1(0, UA)
+        mm1(0, UB)
+        mm1(0, UV)
+        w2_quant(0)
 
-        for r in range(D):
-            e0, e1, e2, e3, e4 = r, r - 1, r - 2, r - 3, r - OUT_LAG
+        for r in range(1, D):
+            e0, e1, e2, e3, e7 = r, r - 1, r - 2, r - 3, r - OUT_LAG
+            sv, vc = split(r)
+            late_gelu = r == 1
             if live(e0 + AHEAD):
                 for g in range(G):
                     load_w1(e0 + AHEAD, g)
-                if 1 <= e0 <= 3:
+                if e0 <= 3:
                     load_w2(e0)
-            if live(e1):
-                w1_quant(e1, UC)
-                mm1(e1, UC)
             if live(e2):
                 h_quant(e2)
                 mm2(e2)
-            if e0 == 0:
-                w1_regroup(e0, UA, nc.scalar.copy)
-                w1_regroup(e0, UV, nc.vector.tensor_copy)
-                w1_regroup(e0, UB, nc.scalar.copy)
-                w1_quant(e0, UA)
-                w1_quant(e0, UV)
-                w1_quant(e0, UB)
-                w1_regroup(e0, UC, nc.scalar.copy)
-                setup()
-                x_scale(e0)
-                w2_regroup(e0)
-                x_quant(e0)
-                mm1(e0, UA)
-                mm1(e0, UB)
-                mm1(e0, UV)
-                w2_quant(e0)
-                continue
-            if live(e0):
-                w1_regroup(e0, UA, nc.scalar.copy)
-                x_scale(e0)
-            if live(e3):
-                ln_var(e3, pow_group(e3))
+            w1_quant(e1, UC)
+            mm1(e1, UC)
+            w1_regroup(e0, UA, s_copy)
+            x_scale(e0)
+            if live(e3) and e3 == pow_group(e3)[1]:
+                ln_rstd(e3)
             if live(e2):
-                ln_mean(e2)
-            if live(e0):
-                w1_regroup(e0, UB, nc.scalar.copy)
-            if live(e1):
+                ln_sum(e2)
+            w1_regroup(e0, UB, s_copy)
+            if not late_gelu:
                 gelu(e1)
-            if live(e0):
-                w1_quant(e0, UA)
+            w1_quant(e0, UA)
             if live(e2):
                 ln_negmean(e2)
-            if live(e0):
-                x_quant(e0)
+            x_quant(e0)
+            if not late_gelu:
                 mm1(e0, UA)
-                if SV_COLS > 0:
-                    w1_regroup(e0, UV, nc.scalar.copy, 0, SV_COLS)
-                w1_regroup(e0, UV, nc.vector.tensor_copy, SV_COLS, H)
-                w1_regroup(e0, UC, nc.scalar.copy, 0, H - VC_COLS)
-                if VC_COLS > 0:
-                    w1_regroup(e0, UC, nc.vector.tensor_copy, H - VC_COLS, H)
-                w1_quant(e0, UB)
-                mm1(e0, UB)
+            w1_regroup(e0, UV, s_copy, 0, sv)
+            w1_regroup(e0, UV, v_copy, sv, H)
+            w1_regroup(e0, UC, s_copy, 0, H - vc)
+            w1_regroup(e0, UC, v_copy, H - vc, H)
+            w1_quant(e0, UB)
+            if late_gelu:
+                gelu(e1)
+                mm1(e0, UA)
+            mm1(e0, UB)
             if live(e2):
                 ln_squares(e2)
-                ln_gain(e2)
-            if live(e4):
-                ln_out(e4)
-            if live(e0):
-                w2_regroup(e0)
-            if live(e1):
-                h_regroup(e1)
-            if live(e0):
-                w1_quant(e0, UV)
-                mm1(e0, UV)
-                w2_quant(e0)
+            if live(e7):
+                ln_gain(e7)
+            w1_quant(e0, UV)
+            mm1(e0, UV)
+            h_regroup(e1)
+            w2_regroup(e0)
+            if live(e7):
+                ln_out(e7)
+            w2_quant(e0)
 
-        w1_quant(D - 1, UC)
-        mm1(D - 1, UC)
-        h_quant(D - 2)
-        mm2(D - 2)
-        ln_var(D - 3, pow_group(D - 3))
-        gelu(D - 1)
-        ln_out(D - 7)
-        ln_mean(D - 2)
-        ln_out(D - 6)
-        ln_negmean(D - 2)
-        ln_squares(D - 2)
-        ln_gain(D - 2)
-        ln_out(D - 5)
-        h_regroup(D - 1)
-        ln_var(D - 2, pow_group(D - 2))
-        ln_out(D - 4)
-        h_quant(D - 1)
-        mm2(D - 1)
-        ln_out(D - 3)
-        ln_mean(D - 1)
-        ln_negmean(D - 1)
-        ln_squares(D - 1)
-        ln_gain(D - 1)
-        ln_out(D - 2)
-        ln_var(D - 1, pow_group(D - 1))
-        ln_out(D - 1)
+        last = D - 1
+        w1_quant(last, UC)
+        mm1(last, UC)
+        h_quant(last - 1)
+        mm2(last - 1)
+        ln_rstd(last - 2)
+        gelu(last)
+        ln_gain(last - 6)
+        ln_out(last - 6)
+        ln_sum(last - 1)
+        ln_gain(last - 5)
+        ln_negmean(last - 1)
+        ln_squares(last - 1)
+        h_regroup(last)
+        ln_out(last - 5)
+        h_quant(last)
+        mm2(last)
+        ln_rstd(last - 1)
+        ln_gain(last - 4)
+        ln_sum(last)
+        ln_out(last - 4)
+        ln_negmean(last)
+        ln_squares(last)
+        ln_gain(last - 3)
+        ln_out(last - 3)
+        ln_gain(last - 2)
+        ln_rstd(last)
+        ln_out(last - 2)
+        ln_gain(last - 1)
+        ln_out(last - 1)
+        ln_gain(last)
+        ln_out(last)

@@ -26,6 +26,7 @@ AHEAD = 2
 UA, UV, UB, UC = 0, 1, 2, 3
 PASS_ORDER = (UA, UB, UV, UC)
 POW_GROUP = 4
+EARLY_B2 = 4
 OUT_LAG = 7
 
 
@@ -275,13 +276,16 @@ def tile_structuralequationmodels_kernel(
 
         cv_v = causal_vars.rearrange("(c p) j v -> p c (j v)", p=P)
         cvr = const.tile([P, BC, K], BF16, name="cvr")
-        adjb = const.tile([P, D * D], BF16, name="adjb")
+        ones_b = const.tile([P, P], BF16, name="ones_b")
+        rowt = const.tile([P, D * D + EARLY_B2 * V], BF16, name="rowt")
         b1t = const.tile([P, P], BF16, name="b1t")
         w2r = const.tile([P, D, PACK, V], BF16, name="w2r")
         b2bc = const.tile([P, D * V], BF16, name="b2bc")
         gbc = const.tile([P, D * V], BF16, name="gbc")
         bbc = const.tile([P, D * V], BF16, name="bbc")
         nc.vector.memset(b1t[:], 0.0)
+        nc.vector.memset(rowt[:], 0.0)
+        nc.vector.memset(ones_b[:], 1.0)
 
         def load_w2(q):
             nc.sync.dma_start(
@@ -295,16 +299,27 @@ def tile_structuralequationmodels_kernel(
         nc.sync.dma_start(out=cvr[:, 0, :], in_=cv_v[:, 0, :])
         load_w1(0, 3)
         nc.sync.dma_start(out=cvr[:, 1, :], in_=cv_v[:, 1, :])
-        nc.sync.dma_start(out=adjb[:], in_=adj_soft.rearrange("i j -> (i j)").partition_broadcast(P))
+        nc.sync.dma_start(out=rowt[0:1, 0 : D * D], in_=adj_soft.rearrange("(o i) j -> o (i j)", o=1))
         nc.sync.dma_start(out=b1t[0 : D * C, :], in_=b1.rearrange("i (c m) -> (i c) m", m=P))
+        nc.sync.dma_start(
+            out=rowt[0:1, D * D :], in_=b2[0:EARLY_B2].rearrange("(o i) v -> o (i v)", o=1)
+        )
         load_w1(1, 0)
         load_w1(1, 1)
         load_w1(1, 2)
         load_w2(0)
         load_w1(1, 3)
-        nc.sync.dma_start(out=b2bc[:], in_=b2.rearrange("i v -> (i v)").partition_broadcast(P))
-        nc.sync.dma_start(out=gbc[:], in_=gamma.rearrange("i v -> (i v)").partition_broadcast(P))
-        nc.sync.dma_start(out=bbc[:], in_=beta.rearrange("i v -> (i v)").partition_broadcast(P))
+
+        def load_spread(r):
+            if r == 2:
+                nc.sync.dma_start(
+                    out=b2bc[:, EARLY_B2 * V :],
+                    in_=b2[EARLY_B2:D].rearrange("i v -> (i v)").partition_broadcast(P),
+                )
+            if r == 3:
+                nc.sync.dma_start(out=gbc[:], in_=gamma.rearrange("i v -> (i v)").partition_broadcast(P))
+            if r == 4:
+                nc.sync.dma_start(out=bbc[:], in_=beta.rearrange("i v -> (i v)").partition_broadcast(P))
 
         ident_f = const.tile([P, P], F32, name="ident_f")
         make_identity(nc, ident_f[:])
@@ -331,11 +346,13 @@ def tile_structuralequationmodels_kernel(
                             ident_f[:],
                         )
                 nc.vector.tensor_copy(out=cvgw[:, g], in_=xt[:].rearrange("p u b -> p b u"))
+            adj_ps = ps_set.tile([P, D * D], F32, name="adj_ps", tag="set")
+            nc.tensor.matmul(out=adj_ps[:], lhsT=ones_b[:], rhs=rowt[:, 0 : D * D], start=True, stop=True)
             for q in range(4):
                 rows = slice(32 * q, 32 * q + 32)
                 nc.vector.tensor_copy(
                     out=adjcol[rows, :].rearrange("p (i g) -> p i g", g=G),
-                    in_=adjb[rows, :].rearrange("p (i g q) -> p i g q", g=G, q=4)[:, :, :, q],
+                    in_=adj_ps[rows, :].rearrange("p (i g q) -> p i g q", g=G, q=4)[:, :, :, q],
                 )
             b1ps = ps_set.tile([P, P], BF16, name="b1ps", tag="set")
             nc.tensor.transpose(b1ps[:], b1t[:], ident_b[:])
@@ -362,6 +379,9 @@ def tile_structuralequationmodels_kernel(
         mm1(0, UB)
         mm1(0, UV)
         w2_quant(0)
+        b2_ps = ps_set.tile([P, EARLY_B2 * V], F32, name="b2_ps", tag="set")
+        nc.tensor.matmul(out=b2_ps[:], lhsT=ones_b[:], rhs=rowt[:, D * D :], start=True, stop=True)
+        nc.vector.tensor_copy(out=b2bc[:, 0 : EARLY_B2 * V], in_=b2_ps[:])
 
         for r in range(1, D):
             e0, e1, e2, e3, e7 = r, r - 1, r - 2, r - 3, r - OUT_LAG
@@ -372,6 +392,7 @@ def tile_structuralequationmodels_kernel(
                     load_w1(e0 + AHEAD, g)
                 if e0 <= 3:
                     load_w2(e0)
+                load_spread(e0)
             if live(e2):
                 h_quant(e2)
                 mm2(e2)

@@ -357,6 +357,9 @@ def tile_structuralequationmodels_kernel(
             b1ps = ps_set.tile([P, P], BF16, name="b1ps", tag="set")
             nc.tensor.transpose(b1ps[:], b1t[:], ident_b[:])
             nc.vector.tensor_copy(out=b1col[:], in_=b1ps[:, 0 : D * C])
+            b2_ps = ps_set.tile([P, EARLY_B2 * V], F32, name="b2_ps", tag="set")
+            nc.tensor.matmul(out=b2_ps[:], lhsT=ones_b[:], rhs=rowt[:, D * D :], start=True, stop=True)
+            T[("b2_ps", 0)] = b2_ps
 
         s_copy = nc.scalar.copy
         v_copy = nc.vector.tensor_copy
@@ -379,9 +382,6 @@ def tile_structuralequationmodels_kernel(
         mm1(0, UB)
         mm1(0, UV)
         w2_quant(0)
-        b2_ps = ps_set.tile([P, EARLY_B2 * V], F32, name="b2_ps", tag="set")
-        nc.tensor.matmul(out=b2_ps[:], lhsT=ones_b[:], rhs=rowt[:, D * D :], start=True, stop=True)
-        nc.vector.tensor_copy(out=b2bc[:, 0 : EARLY_B2 * V], in_=b2_ps[:])
 
         for r in range(1, D):
             e0, e1, e2, e3, e7 = r, r - 1, r - 2, r - 3, r - OUT_LAG
@@ -419,6 +419,7 @@ def tile_structuralequationmodels_kernel(
             w1_regroup(e0, UC, v_copy, H - vc, H)
             w1_quant(e0, UB)
             if late_gelu:
+                nc.scalar.copy(out=b2bc[:, 0 : EARLY_B2 * V], in_=T[("b2_ps", 0)][:])
                 gelu(e1)
                 mm1(e0, UA)
             mm1(e0, UB)

@@ -28,14 +28,16 @@ PASS_ORDER = (UA, UB, UV, UC)
 POW_GROUP = 4
 EARLY_B2 = 4
 OUT_LAG = 7
+PE_COLS = 448
+PE_PART = PE_COLS // 2
 
 
 def split(r):
     if r <= 2:
-        return ((320, 192)[r - 1], 0)
+        return (512, 384)[r - 1]
     if r < OUT_LAG:
-        return (0, 160)
-    return (48, 0)
+        return 48
+    return 256
 
 
 def regroup(copy, dst, src):
@@ -95,6 +97,27 @@ def tile_structuralequationmodels_kernel(
             if ("grp", e, g) not in T:
                 T[("grp", e, g)] = grpp.tile([P, H, PACK], BF16, name="grp", align_bytes=64)
             regroup(copy, T[("grp", e, g)][:, lo:hi, :], T[("raw", e, g)][:, :, lo:hi])
+
+        def pe_regroup(e):
+            for n in range(2):
+                bank = ps_set.tile([P, PE_PART, PACK], BF16, name="bank", tag="set")
+                for m in range(2):
+                    cols = slice(m * PE_PART // 2, (m + 1) * PE_PART // 2)
+                    first = n * PE_PART + m * PE_PART // 2
+                    nc.tensor.matmul(
+                        out=bank[:, cols, :].rearrange("p h t -> p t h"),
+                        lhsT=ident_b[:],
+                        rhs=T[("raw", e, UC)][:, :, first : first + PE_PART // 2],
+                        start=True,
+                        stop=True,
+                    )
+                T[("bank", e, n)] = bank
+
+        def pe_copy_out(e):
+            grp = grpp.tile([P, H, PACK], BF16, name="grp", align_bytes=64)
+            T[("grp", e, UC)] = grp
+            for n in range(2):
+                nc.scalar.copy(out=grp[:, n * PE_PART : (n + 1) * PE_PART, :], in_=T[("bank", e, n)][:])
 
         def w1_quant(e, g):
             if g == PASS_ORDER[0]:
@@ -184,7 +207,7 @@ def tile_structuralequationmodels_kernel(
             )
 
         def mm2(e):
-            yps = ps_y.tile([P, BC, V], F32, name="yps")
+            yps = ps_y.tile([P, BC, V], F32, name="yps", tag="yps")
             for bc in range(BC):
                 nc.tensor.matmul_mx(
                     out=yps[:, bc, :],
@@ -357,7 +380,7 @@ def tile_structuralequationmodels_kernel(
             b1ps = ps_set.tile([P, P], BF16, name="b1ps", tag="set")
             nc.tensor.transpose(b1ps[:], b1t[:], ident_b[:])
             nc.vector.tensor_copy(out=b1col[:], in_=b1ps[:, 0 : D * C])
-            b2_ps = ps_set.tile([P, EARLY_B2 * V], F32, name="b2_ps", tag="set")
+            b2_ps = ps_y.tile([P, EARLY_B2 * V], F32, name="b2_ps", tag="yps")
             nc.tensor.matmul(out=b2_ps[:], lhsT=ones_b[:], rhs=rowt[:, D * D :], start=True, stop=True)
             T[("b2_ps", 0)] = b2_ps
 
@@ -381,11 +404,12 @@ def tile_structuralequationmodels_kernel(
         mm1(0, UA)
         mm1(0, UB)
         mm1(0, UV)
+        pe_regroup(1)
         w2_quant(0)
 
         for r in range(1, D):
             e0, e1, e2, e3, e7 = r, r - 1, r - 2, r - 3, r - OUT_LAG
-            sv, vc = split(r)
+            sv = split(r)
             late_gelu = r == 1
             if live(e0 + AHEAD):
                 for g in range(G):
@@ -415,8 +439,8 @@ def tile_structuralequationmodels_kernel(
                 mm1(e0, UA)
             w1_regroup(e0, UV, s_copy, 0, sv)
             w1_regroup(e0, UV, v_copy, sv, H)
-            w1_regroup(e0, UC, s_copy, 0, H - vc)
-            w1_regroup(e0, UC, v_copy, H - vc, H)
+            pe_copy_out(e0)
+            w1_regroup(e0, UC, v_copy, PE_COLS, H)
             w1_quant(e0, UB)
             if late_gelu:
                 nc.scalar.copy(out=b2bc[:, 0 : EARLY_B2 * V], in_=T[("b2_ps", 0)][:])
@@ -429,6 +453,8 @@ def tile_structuralequationmodels_kernel(
                 ln_gain(e7)
             w1_quant(e0, UV)
             mm1(e0, UV)
+            if live(e0 + 1):
+                pe_regroup(e0 + 1)
             h_regroup(e1)
             w2_regroup(e0)
             if live(e7):

@@ -28,16 +28,16 @@ PASS_ORDER = (UA, UB, UV, UC)
 POW_GROUP = 4
 EARLY_B2 = 4
 OUT_LAG = 7
-PE_COLS = 448
-PE_PART = PE_COLS // 2
+PE_FROM = 3
+PE_PART = H // 2
 
 
 def split(r):
     if r <= 2:
-        return (512, 384)[r - 1]
+        return (320, 192)[r - 1]
     if r < OUT_LAG:
-        return 48
-    return 256
+        return 64
+    return 160
 
 
 def regroup(copy, dst, src):
@@ -404,7 +404,6 @@ def tile_structuralequationmodels_kernel(
         mm1(0, UA)
         mm1(0, UB)
         mm1(0, UV)
-        pe_regroup(1)
         w2_quant(0)
 
         for r in range(1, D):
@@ -439,8 +438,10 @@ def tile_structuralequationmodels_kernel(
                 mm1(e0, UA)
             w1_regroup(e0, UV, s_copy, 0, sv)
             w1_regroup(e0, UV, v_copy, sv, H)
-            pe_copy_out(e0)
-            w1_regroup(e0, UC, v_copy, PE_COLS, H)
+            if e0 >= PE_FROM:
+                pe_copy_out(e0)
+            else:
+                w1_regroup(e0, UC, s_copy)
             w1_quant(e0, UB)
             if late_gelu:
                 nc.scalar.copy(out=b2bc[:, 0 : EARLY_B2 * V], in_=T[("b2_ps", 0)][:])
@@ -453,7 +454,7 @@ def tile_structuralequationmodels_kernel(
                 ln_gain(e7)
             w1_quant(e0, UV)
             mm1(e0, UV)
-            if live(e0 + 1):
+            if PE_FROM <= e0 + 1 < D:
                 pe_regroup(e0 + 1)
             h_regroup(e1)
             w2_regroup(e0)

@@ -421,6 +421,8 @@ def tile_structuralequationmodels_kernel(
                 mm2(e2)
             w1_quant(e1, UC)
             mm1(e1, UC)
+            if e0 >= PE_FROM:
+                pe_regroup(e0)
             w1_regroup(e0, UA, s_copy)
             x_scale(e0)
             if live(e3) and e3 == pow_group(e3)[1]:
@@ -454,8 +456,6 @@ def tile_structuralequationmodels_kernel(
                 ln_gain(e7)
             w1_quant(e0, UV)
             mm1(e0, UV)
-            if PE_FROM <= e0 + 1 < D:
-                pe_regroup(e0 + 1)
             h_regroup(e1)
             w2_regroup(e0)
             if live(e7):

@@ -72,7 +72,7 @@ def tile_structuralequationmodels_kernel(
         xqp = ctx.enter_context(tc.tile_pool(name="xqp", bufs=3))
         hp = ctx.enter_context(tc.tile_pool(name="hp", bufs=3))
         lnp = ctx.enter_context(tc.tile_pool(name="lnp", bufs=3))
-        stp = ctx.enter_context(tc.tile_pool(name="stp", bufs=3))
+        stp = ctx.enter_context(tc.tile_pool(name="stp", bufs=4))
         ps_set = ctx.enter_context(tc.psum_pool(name="ps_set", bufs=2))
         ps_h = ctx.enter_context(tc.psum_pool(name="ps_h", bufs=1))
         ps_y = ctx.enter_context(tc.psum_pool(name="ps_y", bufs=2))
@@ -119,14 +119,14 @@ def tile_structuralequationmodels_kernel(
             for n in range(2):
                 nc.scalar.copy(out=grp[:, n * PE_PART : (n + 1) * PE_PART, :], in_=T[("bank", e, n)][:])
 
-        def w1_quant(e, g):
+        def w1_quant(e, g, lo=0, hi=H):
             if g == PASS_ORDER[0]:
                 T[("w1c", e)] = w1qp.tile([P, G, H], U32, name="w1c", align_bytes=64)
                 T[("w1s", e)] = w1qp.tile([P, G, H], U8, name="w1s", align_bytes=64)
             nc.vector.quantize_mx(
-                out=T[("w1c", e)][:, g, :].bitcast(FP8X4),
-                scales=T[("w1s", e)][:, g, :],
-                in_=T[("grp", e, g)][:].rearrange("p w t -> p (w t)"),
+                out=T[("w1c", e)][:, g, lo:hi].bitcast(FP8X4),
+                scales=T[("w1s", e)][:, g, lo:hi],
+                in_=T[("grp", e, g)][:, lo:hi, :].rearrange("p w t -> p (w t)"),
             )
 
         def x_scale(e):
@@ -150,10 +150,10 @@ def tile_structuralequationmodels_kernel(
                 in_=T[("xs", e)][:].rearrange("p g e -> p (g e)"),
             )
 
-        def mm1(e, g):
+        def mm1(e, g, chunks=range(C)):
             first = g == PASS_ORDER[0]
             last = g == PASS_ORDER[-1]
-            for c in range(C):
+            for c in chunks:
                 if first:
                     T[("hps", e, c)] = ps_h.tile([P, B], F32, name="hps%d" % c)
                 nc.tensor.matmul_mx(
@@ -166,45 +166,49 @@ def tile_structuralequationmodels_kernel(
                     stop=last,
                 )
 
-        def gelu(e):
-            ht = hp.tile([P, C, B], BF16, name="ht")
-            for c in range(C):
+        def gelu(e, chunks=range(C), lo=0, hi=B):
+            if ("ht", e) not in T:
+                T[("ht", e)] = hp.tile([P, C, B], BF16, name="ht")
+            for c in chunks:
                 nc.scalar.activation(
-                    out=ht[:, c, :],
-                    in_=T[("hps", e, c)][:],
+                    out=T[("ht", e)][:, c, lo:hi],
+                    in_=T[("hps", e, c)][:, lo:hi],
                     func=ACT.Gelu,
                     bias=b1col[:, C * e + c : C * e + c + 1],
                     scale=1.0,
                 )
-            T[("ht", e)] = ht
 
-        def h_regroup(e):
-            hg = hp.tile([P, B, PACK], BF16, name="hg", align_bytes=64)
-            regroup(nc.vector.tensor_copy, hg[:], T[("ht", e)][:])
-            T[("hg", e)] = hg
+        def h_regroup(e, copy, lo=0, hi=B):
+            if ("hg", e) not in T:
+                T[("hg", e)] = hp.tile([P, B, PACK], BF16, name="hg", align_bytes=64)
+            regroup(copy, T[("hg", e)][:, lo:hi, :], T[("ht", e)][:, :, lo:hi])
 
-        def h_quant(e):
-            T[("hc", e)] = hp.tile([P, B], U32, name="hc", align_bytes=64)
-            T[("hs", e)] = hp.tile([P, B], U8, name="hs", align_bytes=64)
+        def h_quant(e, lo=0, hi=B):
+            if ("hc", e) not in T:
+                T[("hc", e)] = hp.tile([P, B], U32, name="hc", align_bytes=64)
+                T[("hs", e)] = hp.tile([P, B], U8, name="hs", align_bytes=64)
             nc.vector.quantize_mx(
-                out=T[("hc", e)][:].bitcast(FP8X4),
-                scales=T[("hs", e)][:],
-                in_=T[("hg", e)][:].rearrange("p w t -> p (w t)"),
+                out=T[("hc", e)][:, lo:hi].bitcast(FP8X4),
+                scales=T[("hs", e)][:, lo:hi],
+                in_=T[("hg", e)][:, lo:hi, :].rearrange("p w t -> p (w t)"),
             )
 
         def w2_regroup(e):
-            g2 = hp.tile([P, V, PACK], BF16, name="g2", align_bytes=64)
-            regroup(nc.vector.tensor_copy, g2[:], w2r[:, e])
+            g2 = hp.tile([P, 2 * V, PACK], BF16, name="g2", align_bytes=64)
+            regroup(nc.vector.tensor_copy, g2[:], w2r[:, :, e : e + 2, :].rearrange("p t i v -> p t (i v)"))
             T[("g2", e)] = g2
 
         def w2_quant(e):
-            T[("w2c", e)] = hp.tile([P, V], U32, name="w2c", align_bytes=64)
-            T[("w2s", e)] = hp.tile([P, V], U8, name="w2s", align_bytes=64)
+            w2c = hp.tile([P, 2 * V], U32, name="w2c", align_bytes=64)
+            w2s = hp.tile([P, 2 * V], U8, name="w2s", align_bytes=64)
             nc.vector.quantize_mx(
-                out=T[("w2c", e)][:].bitcast(FP8X4),
-                scales=T[("w2s", e)][:],
+                out=w2c[:].bitcast(FP8X4),
+                scales=w2s[:],
                 in_=T[("g2", e)][:].rearrange("p w t -> p (w t)"),
             )
+            for m in range(2):
+                T[("w2c", e + m)] = w2c[:, m * V : (m + 1) * V]
+                T[("w2s", e + m)] = w2s[:, m * V : (m + 1) * V]
 
         def mm2(e):
             yps = ps_y.tile([P, BC, V], F32, name="yps", tag="yps")
@@ -213,17 +217,20 @@ def tile_structuralequationmodels_kernel(
                     out=yps[:, bc, :],
                     lhsT=T[("hc", e)][:, bc * P : (bc + 1) * P].bitcast(FP8X4),
                     lhsT_scale=T[("hs", e)][:, bc * P : (bc + 1) * P],
-                    rhs=T[("w2c", e)][:].bitcast(FP8X4),
-                    rhs_scale=T[("w2s", e)][:],
+                    rhs=T[("w2c", e)].bitcast(FP8X4),
+                    rhs_scale=T[("w2s", e)],
                     start=True,
                     stop=True,
                 )
             T[("yps", e)] = yps
 
         def ln_sum(e):
+            first, last = pow_group(e)
+            if e == first:
+                T[("sz", first)] = stp.tile([P, (last - first + 1) * BC], F32, name="sz")
             z = lnp.tile([P, BC, V], F32, name="z", bufs=OUT_LAG)
-            sz = stp.tile([P, BC], F32, name="sz")
             for bc in range(BC):
+                at = (e - first) * BC + bc
                 nc.vector.scalar_tensor_tensor(
                     out=z[:, bc, :],
                     in0=T[("yps", e)][:, bc, :],
@@ -231,17 +238,18 @@ def tile_structuralequationmodels_kernel(
                     in1=b2bc[:, e * V : (e + 1) * V],
                     op0=ALU.mult,
                     op1=ALU.add,
-                    accum_out=sz[:, bc : bc + 1],
+                    accum_out=T[("sz", first)][:, at : at + 1],
                 )
             T[("z", e)] = z
-            T[("sz", e)] = sz
 
         def ln_negmean(e):
-            nm = stp.tile([P, BC], F32, name="nm", bufs=OUT_LAG)
+            first, last = pow_group(e)
+            nm = stp.tile([P, (last - first + 1) * BC], F32, name="nm")
             nc.vector.tensor_scalar(
-                out=nm[:], in0=T[("sz", e)][:], scalar1=-1.0 / V, scalar2=None, op0=ALU.mult
+                out=nm[:], in0=T[("sz", first)][:], scalar1=-1.0 / V, scalar2=None, op0=ALU.mult
             )
-            T[("nm", e)] = nm
+            for m in range(first, last + 1):
+                T[("nm", m)] = nm[:, (m - first) * BC : (m - first + 1) * BC]
 
         def ln_squares(e):
             first, last = pow_group(e)
@@ -254,8 +262,8 @@ def tile_structuralequationmodels_kernel(
                     out=junk[:],
                     in_=T[("z", e)][:, bc, :],
                     func=ACT.Square,
-                    bias=T[("nm", e)][:, bc : bc + 1],
-                    scale=1.0,
+                    bias=T[("sz", first)][:, at : at + 1],
+                    scale=-float(V),
                     accum_out=T[("ssq", first)][:, at : at + 1],
                 )
 
@@ -264,12 +272,19 @@ def tile_structuralequationmodels_kernel(
             width = (last - first + 1) * BC
             ve = stp.tile([P, width], F32, name="ve")
             nc.vector.tensor_scalar(
-                out=ve[:], in0=T[("ssq", first)][:], scalar1=1.0 / V, scalar2=LN_EPS, op0=ALU.mult, op1=ALU.add
+                out=ve[:], in0=T[("ssq", first)][:], scalar1=1.0 / V**3, scalar2=LN_EPS, op0=ALU.mult, op1=ALU.add
             )
             rstd = stp.tile([P, width], F32, name="rstd")
             nc.gpsimd.tensor_tensor(out=rstd[:], in0=ve[:], in1=negh[:, 0:width], op=ALU.pow)
             for m in range(first, last + 1):
                 T[("rstd", m)] = rstd[:, (m - first) * BC : (m - first + 1) * BC]
+
+        def ln_rstd_scalar(e):
+            rstd = stp.tile([P, BC], F32, name="rstd1")
+            nc.scalar.activation(
+                out=rstd[:], in_=T[("ssq", e)][:], func=ACT.Abs_reciprocal_sqrt, bias=LN_EPS, scale=1.0 / V**3
+            )
+            T[("rstd", e)] = rstd
 
         def ln_gain(e):
             tt = lnp.tile([P, BC, V], F32, name="tt")
@@ -302,7 +317,7 @@ def tile_structuralequationmodels_kernel(
         ones_b = const.tile([P, P], BF16, name="ones_b")
         rowt = const.tile([P, D * D + EARLY_B2 * V], BF16, name="rowt")
         b1t = const.tile([P, P], BF16, name="b1t")
-        w2r = const.tile([P, D, PACK, V], BF16, name="w2r")
+        w2r = const.tile([P, PACK, D, V], BF16, name="w2r")
         b2bc = const.tile([P, D * V], BF16, name="b2bc")
         gbc = const.tile([P, D * V], BF16, name="gbc")
         bbc = const.tile([P, D * V], BF16, name="bbc")
@@ -311,10 +326,11 @@ def tile_structuralequationmodels_kernel(
         nc.vector.memset(ones_b[:], 1.0)
 
         def load_w2(q):
-            nc.sync.dma_start(
-                out=w2r[:, 4 * q : 4 * q + 4],
-                in_=W2[4 * q : 4 * q + 4].rearrange("i (t p) v -> p i t v", p=P),
-            )
+            for t in range(PACK):
+                nc.sync.dma_start(
+                    out=w2r[:, t, 4 * q : 4 * q + 4, :],
+                    in_=W2[4 * q : 4 * q + 4, t * P : (t + 1) * P, :].rearrange("i p v -> p i v"),
+                )
 
         load_w1(0, 0, pieces=2)
         load_w1(0, 1)
@@ -426,6 +442,7 @@ def tile_structuralequationmodels_kernel(
             w1_regroup(e0, UA, s_copy)
             x_scale(e0)
             if live(e3) and e3 == pow_group(e3)[1]:
+                ln_negmean(e3)
                 ln_rstd(e3)
             if live(e2):
                 ln_sum(e2)
@@ -433,8 +450,6 @@ def tile_structuralequationmodels_kernel(
             if not late_gelu:
                 gelu(e1)
             w1_quant(e0, UA)
-            if live(e2):
-                ln_negmean(e2)
             x_quant(e0)
             if not late_gelu:
                 mm1(e0, UA)
@@ -456,39 +471,48 @@ def tile_structuralequationmodels_kernel(
                 ln_gain(e7)
             w1_quant(e0, UV)
             mm1(e0, UV)
-            h_regroup(e1)
-            w2_regroup(e0)
+            h_regroup(e1, v_copy)
+            if e0 % 2 == 0:
+                w2_regroup(e0)
             if live(e7):
                 ln_out(e7)
-            w2_quant(e0)
+            if e0 % 2 == 0:
+                w2_quant(e0)
 
         last = D - 1
-        w1_quant(last, UC)
-        mm1(last, UC)
+        for n in range(2):
+            w1_quant(last, UC, n * H // 2, (n + 1) * H // 2)
+            mm1(last, UC, range(2 * n, 2 * n + 2))
+        gelu(last, range(0, 2))
+        for bc in range(BC):
+            gelu(last, range(2, 4), bc * P, (bc + 1) * P)
         h_quant(last - 1)
         mm2(last - 1)
+        ln_negmean(last - 2)
         ln_rstd(last - 2)
-        gelu(last)
         ln_gain(last - 6)
         ln_out(last - 6)
+        h_regroup(last, v_copy, 0, P)
+        h_regroup(last, s_copy, P, B)
         ln_sum(last - 1)
-        ln_gain(last - 5)
-        ln_negmean(last - 1)
-        ln_squares(last - 1)
-        h_regroup(last)
-        ln_out(last - 5)
-        h_quant(last)
+        for bc in range(BC):
+            h_quant(last, bc * P, (bc + 1) * P)
         mm2(last)
-        ln_rstd(last - 1)
+        nc.scalar.activation(out=warm[:], in_=negh[:, 0:1], func=ACT.Abs_reciprocal_sqrt)
+        ln_gain(last - 5)
+        ln_out(last - 5)
+        ln_squares(last - 1)
+        ln_negmean(last - 1)
+        ln_rstd_scalar(last - 1)
         ln_gain(last - 4)
-        ln_sum(last)
         ln_out(last - 4)
-        ln_negmean(last)
+        ln_sum(last)
         ln_squares(last)
+        ln_rstd_scalar(last)
+        ln_negmean(last)
         ln_gain(last - 3)
         ln_out(last - 3)
         ln_gain(last - 2)
-        ln_rstd(last)
         ln_out(last - 2)
         ln_gain(last - 1)
         ln_out(last - 1)

@@ -33,8 +33,6 @@ PE_PART = H // 2
 
 
 def split(r):
-    if r <= 2:
-        return (320, 192)[r - 1]
     if r < OUT_LAG:
         return 64
     return 160
@@ -81,15 +79,22 @@ def tile_structuralequationmodels_kernel(
         T = {}
         out_v = out.rearrange("(c p) i v -> p c i v", p=P)
 
-        def load_w1(e, g, pieces=1):
-            raw = rawp.tile([P, PACK, H], BF16, name="raw")
+        def load_w1(e, g):
+            T[("raw", e, g)] = rawp.tile([P, PACK, H], BF16, name="raw")
             rows = W1[e][g * K_PASS : (g + 1) * K_PASS, :].rearrange("(p t) h -> p t h", t=PACK)
-            width = H // pieces
-            for n in range(pieces):
-                nc.sync.dma_start(
-                    out=raw[:, :, n * width : (n + 1) * width], in_=rows[:, :, n * width : (n + 1) * width]
-                )
-            T[("raw", e, g)] = raw
+            nc.sync.dma_start(out=T[("raw", e, g)][:], in_=rows)
+
+        def load_halves(g, n):
+            if ("raw", 0, g) not in T:
+                T[("raw", 0, g)] = rawp.tile([P, 2, PACK, H // 2], BF16, name="raw2", tag="raw")
+            rows = W1[0][g * K_PASS : (g + 1) * K_PASS, :].rearrange("(p t) h -> p t h", t=PACK)
+            nc.sync.dma_start(out=T[("raw", 0, g)][:, n], in_=rows[:, :, n * H // 2 : (n + 1) * H // 2])
+
+        def regroup_halves(g, n):
+            if ("grp", 0, g) not in T:
+                T[("grp", 0, g)] = grpp.tile([P, H, PACK], BF16, name="grp", align_bytes=64)
+            dst = T[("grp", 0, g)][:, n * H // 2 : (n + 1) * H // 2, :]
+            regroup(nc.scalar.copy, dst, T[("raw", 0, g)][:, n])
 
         def w1_regroup(e, g, copy, lo=0, hi=H):
             if hi <= lo:
@@ -129,25 +134,26 @@ def tile_structuralequationmodels_kernel(
                 in_=T[("grp", e, g)][:, lo:hi, :].rearrange("p w t -> p (w t)"),
             )
 
-        def x_scale(e):
-            xs = xp.tile([P, G, B * PACK], BF16, name="xs", align_bytes=64)
-            for g in range(G):
+        def x_scale(e, passes=range(G)):
+            if ("xs", e) not in T:
+                T[("xs", e)] = xp.tile([P, G, B * PACK], BF16, name="xs", align_bytes=64)
+            for g in passes:
                 nc.vector.tensor_scalar(
-                    out=xs[:, g, :],
+                    out=T[("xs", e)][:, g, :],
                     in0=cvg[:, g].rearrange("p b t -> p (b t)"),
                     scalar1=adjcol[:, G * e + g : G * e + g + 1],
                     scalar2=None,
                     op0=ALU.mult,
                 )
-            T[("xs", e)] = xs
 
-        def x_quant(e):
-            T[("xc", e)] = xqp.tile([P, G * B], U32, name="xc", align_bytes=64)
-            T[("xsc", e)] = xqp.tile([P, G * B], U8, name="xsc", align_bytes=64)
+        def x_quant(e, lo=0, hi=G):
+            if ("xc", e) not in T:
+                T[("xc", e)] = xqp.tile([P, G * B], U32, name="xc", align_bytes=64)
+                T[("xsc", e)] = xqp.tile([P, G * B], U8, name="xsc", align_bytes=64)
             nc.vector.quantize_mx(
-                out=T[("xc", e)][:].bitcast(FP8X4),
-                scales=T[("xsc", e)][:],
-                in_=T[("xs", e)][:].rearrange("p g e -> p (g e)"),
+                out=T[("xc", e)][:, lo * B : hi * B].bitcast(FP8X4),
+                scales=T[("xsc", e)][:, lo * B : hi * B],
+                in_=T[("xs", e)][:, lo:hi, :].rearrange("p g e -> p (g e)"),
             )
 
         def mm1(e, g, chunks=range(C)):
@@ -167,11 +173,11 @@ def tile_structuralequationmodels_kernel(
                 )
 
         def gelu(e, chunks=range(C), lo=0, hi=B):
-            if ("ht", e) not in T:
-                T[("ht", e)] = hp.tile([P, C, B], BF16, name="ht")
+            if ("ht", e, lo) not in T:
+                T[("ht", e, lo)] = hp.tile([P, C, hi - lo], BF16, name="ht")
             for c in chunks:
                 nc.scalar.activation(
-                    out=T[("ht", e)][:, c, lo:hi],
+                    out=T[("ht", e, lo)][:, c, :],
                     in_=T[("hps", e, c)][:, lo:hi],
                     func=ACT.Gelu,
                     bias=b1col[:, C * e + c : C * e + c + 1],
@@ -181,7 +187,7 @@ def tile_structuralequationmodels_kernel(
         def h_regroup(e, copy, lo=0, hi=B):
             if ("hg", e) not in T:
                 T[("hg", e)] = hp.tile([P, B, PACK], BF16, name="hg", align_bytes=64)
-            regroup(copy, T[("hg", e)][:, lo:hi, :], T[("ht", e)][:, :, lo:hi])
+            regroup(copy, T[("hg", e)][:, lo:hi, :], T[("ht", e, lo)][:])
 
         def h_quant(e, lo=0, hi=B):
             if ("hc", e) not in T:
@@ -195,7 +201,8 @@ def tile_structuralequationmodels_kernel(
 
         def w2_regroup(e):
             g2 = hp.tile([P, 2 * V, PACK], BF16, name="g2", align_bytes=64)
-            regroup(nc.vector.tensor_copy, g2[:], w2r[:, :, e : e + 2, :].rearrange("p t i v -> p t (i v)"))
+            src = w2r[e // 4][:, :, e % 4 : e % 4 + 2, :]
+            regroup(nc.vector.tensor_copy, g2[:], src.rearrange("p t i v -> p t (i v)"))
             T[("g2", e)] = g2
 
         def w2_quant(e):
@@ -313,41 +320,49 @@ def tile_structuralequationmodels_kernel(
             nc.sync.dma_start(out=out_v[:, :, e, :], in_=o[:])
 
         cv_v = causal_vars.rearrange("(c p) j v -> p c (j v)", p=P)
-        cvr = const.tile([P, BC, K], BF16, name="cvr")
+        cvr = [const.tile([P, BC, K_PASS], BF16, name="cvr%d" % g) for g in range(G)]
         ones_b = const.tile([P, P], BF16, name="ones_b")
         rowt = const.tile([P, D * D + EARLY_B2 * V], BF16, name="rowt")
         b1t = const.tile([P, P], BF16, name="b1t")
-        w2r = const.tile([P, PACK, D, V], BF16, name="w2r")
+        w2r = [const.tile([P, PACK, 4, V], BF16, name="w2r%d" % q) for q in range(D // 4)]
         b2bc = const.tile([P, D * V], BF16, name="b2bc")
         gbc = const.tile([P, D * V], BF16, name="gbc")
         bbc = const.tile([P, D * V], BF16, name="bbc")
-        nc.vector.memset(b1t[:], 0.0)
         nc.vector.memset(rowt[:], 0.0)
         nc.vector.memset(ones_b[:], 1.0)
+        nc.vector.memset(b1t[:], 0.0)
 
         def load_w2(q):
             for t in range(PACK):
                 nc.sync.dma_start(
-                    out=w2r[:, t, 4 * q : 4 * q + 4, :],
+                    out=w2r[q][:, t],
                     in_=W2[4 * q : 4 * q + 4, t * P : (t + 1) * P, :].rearrange("i p v -> p i v"),
                 )
 
-        load_w1(0, 0, pieces=2)
-        load_w1(0, 1)
-        load_w1(0, 2)
-        nc.sync.dma_start(out=cvr[:, 0, :], in_=cv_v[:, 0, :])
-        load_w1(0, 3)
-        nc.sync.dma_start(out=cvr[:, 1, :], in_=cv_v[:, 1, :])
+        def load_x(g):
+            cols = slice(g * K_PASS, (g + 1) * K_PASS)
+            nc.sync.dma_start(out=cvr[g][:], in_=cv_v[:, :, cols])
+
+        load_x(0)
+        load_halves(UA, 0)
         nc.sync.dma_start(out=rowt[0:1, 0 : D * D], in_=adj_soft.rearrange("(o i) j -> o (i j)", o=1))
+        load_x(1)
+        load_halves(UA, 1)
+        load_x(2)
+        load_halves(UB, 0)
+        load_x(3)
+        load_halves(UB, 1)
+        load_w1(0, UC)
+        load_w1(0, UV)
         nc.sync.dma_start(out=b1t[0 : D * C, :], in_=b1.rearrange("i (c m) -> (i c) m", m=P))
         nc.sync.dma_start(
             out=rowt[0:1, D * D :], in_=b2[0:EARLY_B2].rearrange("(o i) v -> o (i v)", o=1)
         )
-        load_w1(1, 0)
-        load_w1(1, 1)
-        load_w1(1, 2)
+        load_w1(1, UA)
+        load_w1(1, UB)
+        load_w1(1, UV)
         load_w2(0)
-        load_w1(1, 3)
+        load_w1(1, UC)
 
         def load_spread(r):
             if r == 2:
@@ -372,19 +387,23 @@ def tile_structuralequationmodels_kernel(
         b1col = const.tile([P, D * C], F32, name="b1col")
         cvg = const.tile([P, G, B, PACK], BF16, name="cvg", align_bytes=64)
 
-        def setup():
-            cvw = cvr[:].bitcast(F32)
+        def x_turn(g):
+            cvw = cvr[g][:].bitcast(F32)
+            xt = ps_set.tile([P, 2, B], F32, name="xt", tag="set")
+            for bc in range(BC):
+                for u in range(2):
+                    nc.tensor.transpose(
+                        xt[:, u, bc * P : (bc + 1) * P],
+                        cvw[:, bc, u::2],
+                        ident_f[:],
+                    )
+            T[("xt", g)] = xt
+
+        def x_copy(g):
             cvgw = cvg[:].bitcast(F32)
-            for g in range(G):
-                xt = ps_set.tile([P, 2, B], F32, name="xt", tag="set")
-                for bc in range(BC):
-                    for u in range(2):
-                        nc.tensor.transpose(
-                            xt[:, u, bc * P : (bc + 1) * P],
-                            cvw[:, bc, 256 * g + u : 256 * (g + 1) : 2],
-                            ident_f[:],
-                        )
-                nc.vector.tensor_copy(out=cvgw[:, g], in_=xt[:].rearrange("p u b -> p b u"))
+            nc.vector.tensor_copy(out=cvgw[:, g], in_=T[("xt", g)][:].rearrange("p u b -> p b u"))
+
+        def adj_spread():
             adj_ps = ps_set.tile([P, D * D], F32, name="adj_ps", tag="set")
             nc.tensor.matmul(out=adj_ps[:], lhsT=ones_b[:], rhs=rowt[:, 0 : D * D], start=True, stop=True)
             for q in range(4):
@@ -393,6 +412,8 @@ def tile_structuralequationmodels_kernel(
                     out=adjcol[rows, :].rearrange("p (i g) -> p i g", g=G),
                     in_=adj_ps[rows, :].rearrange("p (i g q) -> p i g q", g=G, q=4)[:, :, :, q],
                 )
+
+        def bias_spread():
             b1ps = ps_set.tile([P, P], BF16, name="b1ps", tag="set")
             nc.tensor.transpose(b1ps[:], b1t[:], ident_b[:])
             nc.vector.tensor_copy(out=b1col[:], in_=b1ps[:, 0 : D * C])
@@ -405,27 +426,40 @@ def tile_structuralequationmodels_kernel(
 
         for g in range(G):
             load_w1(AHEAD, g)
-        w1_regroup(0, UA, s_copy, 0, H // 2)
-        w1_regroup(0, UA, s_copy, H // 2, H)
-        w1_regroup(0, UV, v_copy)
-        w1_regroup(0, UB, s_copy)
-        w1_quant(0, UA)
-        w1_quant(0, UV)
-        w1_quant(0, UB)
+        for n in range(2):
+            regroup_halves(UA, n)
+        for n in range(2):
+            regroup_halves(UB, n)
         w1_regroup(0, UC, s_copy)
-        setup()
-        x_scale(0)
-        w2_regroup(0)
-        x_quant(0)
+        x_turn(0)
+        x_copy(0)
+        adj_spread()
+        x_turn(1)
+        x_scale(0, (0,))
+        x_copy(1)
+        x_quant(0, 0, 1)
+        x_scale(0, (1,))
+        x_turn(2)
+        w1_quant(0, UA)
+        x_copy(2)
+        x_quant(0, 1, 2)
+        x_scale(0, (2,))
+        x_turn(3)
+        x_copy(3)
+        x_quant(0, 2, 3)
+        x_scale(0, (3,))
+        w1_quant(0, UB)
+        x_quant(0, 3, 4)
         mm1(0, UA)
         mm1(0, UB)
+        w1_regroup(0, UV, v_copy)
+        bias_spread()
+        w1_quant(0, UV)
         mm1(0, UV)
-        w2_quant(0)
 
         for r in range(1, D):
             e0, e1, e2, e3, e7 = r, r - 1, r - 2, r - 3, r - OUT_LAG
             sv = split(r)
-            late_gelu = r == 1
             if live(e0 + AHEAD):
                 for g in range(G):
                     load_w1(e0 + AHEAD, g)
@@ -447,12 +481,10 @@ def tile_structuralequationmodels_kernel(
             if live(e2):
                 ln_sum(e2)
             w1_regroup(e0, UB, s_copy)
-            if not late_gelu:
-                gelu(e1)
+            gelu(e1)
             w1_quant(e0, UA)
             x_quant(e0)
-            if not late_gelu:
-                mm1(e0, UA)
+            mm1(e0, UA)
             w1_regroup(e0, UV, s_copy, 0, sv)
             w1_regroup(e0, UV, v_copy, sv, H)
             if e0 >= PE_FROM:
@@ -460,10 +492,8 @@ def tile_structuralequationmodels_kernel(
             else:
                 w1_regroup(e0, UC, s_copy)
             w1_quant(e0, UB)
-            if late_gelu:
+            if e0 == 1:
                 nc.scalar.copy(out=b2bc[:, 0 : EARLY_B2 * V], in_=T[("b2_ps", 0)][:])
-                gelu(e1)
-                mm1(e0, UA)
             mm1(e0, UB)
             if live(e2):
                 ln_squares(e2)
@@ -472,20 +502,21 @@ def tile_structuralequationmodels_kernel(
             w1_quant(e0, UV)
             mm1(e0, UV)
             h_regroup(e1, v_copy)
-            if e0 % 2 == 0:
-                w2_regroup(e0)
+            pair = 0 if e0 == 1 else e0
+            if pair % 2 == 0:
+                w2_regroup(pair)
             if live(e7):
                 ln_out(e7)
-            if e0 % 2 == 0:
-                w2_quant(e0)
+            if pair % 2 == 0:
+                w2_quant(pair)
 
         last = D - 1
         for n in range(2):
             w1_quant(last, UC, n * H // 2, (n + 1) * H // 2)
             mm1(last, UC, range(2 * n, 2 * n + 2))
-        gelu(last, range(0, 2))
-        for bc in range(BC):
-            gelu(last, range(2, 4), bc * P, (bc + 1) * P)
+        for chunks in (range(0, 2), range(2, 4)):
+            for bc in range(BC):
+                gelu(last, chunks, bc * P, (bc + 1) * P)
         h_quant(last - 1)
         mm2(last - 1)
         ln_negmean(last - 2)

@@ -25,17 +25,14 @@ FLOPS = 2 * B * D * (K * H + H * V)
 AHEAD = 2
 UA, UV, UB, UC = 0, 1, 2, 3
 PASS_ORDER = (UA, UB, UV, UC)
-POW_GROUP = 4
 EARLY_B2 = 4
-OUT_LAG = 7
+OUT_FROM = 11
 PE_FROM = 3
 PE_PART = H // 2
 
 
 def split(r):
-    if r < OUT_LAG:
-        return 64
-    return 160
+    return 88 if r < OUT_FROM else 224
 
 
 def regroup(copy, dst, src):
@@ -45,12 +42,16 @@ def regroup(copy, dst, src):
     )
 
 
-def pow_group(e):
-    if e < D - 4:
-        return (e - e % POW_GROUP, e - e % POW_GROUP + POW_GROUP - 1)
+def group(e):
+    if e < D // 2:
+        return (0, D // 2 - 1)
     if e < D - 2:
-        return (D - 4, D - 3)
+        return (D // 2, D - 3)
     return (e, e)
+
+
+def finished(r):
+    return [e for e in range(D // 2) if OUT_FROM + e * (D - OUT_FROM) // (D // 2) == r]
 
 
 def live(e):
@@ -232,10 +233,10 @@ def tile_structuralequationmodels_kernel(
             T[("yps", e)] = yps
 
         def ln_sum(e):
-            first, last = pow_group(e)
+            first, last = group(e)
             if e == first:
                 T[("sz", first)] = stp.tile([P, (last - first + 1) * BC], F32, name="sz")
-            z = lnp.tile([P, BC, V], F32, name="z", bufs=OUT_LAG)
+            z = lnp.tile([P, BC, V], F32, name="z", bufs=10)
             for bc in range(BC):
                 at = (e - first) * BC + bc
                 nc.vector.scalar_tensor_tensor(
@@ -250,7 +251,7 @@ def tile_structuralequationmodels_kernel(
             T[("z", e)] = z
 
         def ln_negmean(e):
-            first, last = pow_group(e)
+            first, last = group(e)
             nm = stp.tile([P, (last - first + 1) * BC], F32, name="nm")
             nc.vector.tensor_scalar(
                 out=nm[:], in0=T[("sz", first)][:], scalar1=-1.0 / V, scalar2=None, op0=ALU.mult
@@ -259,7 +260,7 @@ def tile_structuralequationmodels_kernel(
                 T[("nm", m)] = nm[:, (m - first) * BC : (m - first + 1) * BC]
 
         def ln_squares(e):
-            first, last = pow_group(e)
+            first, last = group(e)
             if e == first:
                 T[("ssq", first)] = stp.tile([P, (last - first + 1) * BC], F32, name="ssq")
             for bc in range(BC):
@@ -275,7 +276,7 @@ def tile_structuralequationmodels_kernel(
                 )
 
         def ln_rstd(e):
-            first, last = pow_group(e)
+            first, last = group(e)
             width = (last - first + 1) * BC
             ve = stp.tile([P, width], F32, name="ve")
             nc.vector.tensor_scalar(
@@ -287,14 +288,16 @@ def tile_structuralequationmodels_kernel(
                 T[("rstd", m)] = rstd[:, (m - first) * BC : (m - first + 1) * BC]
 
         def ln_rstd_scalar(e):
-            rstd = stp.tile([P, BC], F32, name="rstd1")
+            first, last = group(e)
+            rstd = stp.tile([P, (last - first + 1) * BC], F32, name="rstd1")
             nc.scalar.activation(
-                out=rstd[:], in_=T[("ssq", e)][:], func=ACT.Abs_reciprocal_sqrt, bias=LN_EPS, scale=1.0 / V**3
+                out=rstd[:], in_=T[("ssq", first)][:], func=ACT.Abs_reciprocal_sqrt, bias=LN_EPS, scale=1.0 / V**3
             )
-            T[("rstd", e)] = rstd
+            for m in range(first, last + 1):
+                T[("rstd", m)] = rstd[:, (m - first) * BC : (m - first + 1) * BC]
 
         def ln_gain(e):
-            tt = lnp.tile([P, BC, V], F32, name="tt")
+            tt = lnp.tile([P, BC, V], F32, name="tt", bufs=6)
             for bc in range(BC):
                 nc.vector.scalar_tensor_tensor(
                     out=tt[:, bc, :],
@@ -379,7 +382,7 @@ def tile_structuralequationmodels_kernel(
         make_identity(nc, ident_f[:])
         ident_b = const.tile([P, P], BF16, name="ident_b")
         make_identity(nc, ident_b[:])
-        negh = const.tile([P, POW_GROUP * BC], F32, name="negh")
+        negh = const.tile([P, D // 2 * BC], F32, name="negh")
         nc.vector.memset(negh[:], -0.5)
         warm = const.tile([P, 1], F32, name="warm")
         nc.scalar.activation(out=warm[:], in_=negh[:, 0:1], func=ACT.Gelu)
@@ -458,7 +461,7 @@ def tile_structuralequationmodels_kernel(
         mm1(0, UV)
 
         for r in range(1, D):
-            e0, e1, e2, e3, e7 = r, r - 1, r - 2, r - 3, r - OUT_LAG
+            e0, e1, e2, e3 = r, r - 1, r - 2, r - 3
             sv = split(r)
             if live(e0 + AHEAD):
                 for g in range(G):
@@ -475,7 +478,7 @@ def tile_structuralequationmodels_kernel(
                 pe_regroup(e0)
             w1_regroup(e0, UA, s_copy)
             x_scale(e0)
-            if live(e3) and e3 == pow_group(e3)[1]:
+            if live(e3) and e3 == group(e3)[1]:
                 ln_negmean(e3)
                 ln_rstd(e3)
             if live(e2):
@@ -497,16 +500,16 @@ def tile_structuralequationmodels_kernel(
             mm1(e0, UB)
             if live(e2):
                 ln_squares(e2)
-            if live(e7):
-                ln_gain(e7)
+            for e in finished(r):
+                ln_gain(e)
             w1_quant(e0, UV)
             mm1(e0, UV)
             h_regroup(e1, v_copy)
             pair = 0 if e0 == 1 else e0
             if pair % 2 == 0:
                 w2_regroup(pair)
-            if live(e7):
-                ln_out(e7)
+            for e in finished(r):
+                ln_out(e)
             if pair % 2 == 0:
                 w2_quant(pair)
 
@@ -520,32 +523,32 @@ def tile_structuralequationmodels_kernel(
         h_quant(last - 1)
         mm2(last - 1)
         ln_negmean(last - 2)
-        ln_rstd(last - 2)
+        ln_gain(last - 7)
         ln_gain(last - 6)
-        ln_out(last - 6)
         h_regroup(last, v_copy, 0, P)
         h_regroup(last, s_copy, P, B)
+        nc.scalar.activation(out=warm[:], in_=negh[:, 0:1], func=ACT.Abs_reciprocal_sqrt)
+        ln_rstd_scalar(last - 2)
         ln_sum(last - 1)
+        ln_squares(last - 1)
+        ln_rstd_scalar(last - 1)
+        ln_gain(last - 5)
         for bc in range(BC):
             h_quant(last, bc * P, (bc + 1) * P)
         mm2(last)
-        nc.scalar.activation(out=warm[:], in_=negh[:, 0:1], func=ACT.Abs_reciprocal_sqrt)
-        ln_gain(last - 5)
-        ln_out(last - 5)
-        ln_squares(last - 1)
-        ln_negmean(last - 1)
-        ln_rstd_scalar(last - 1)
         ln_gain(last - 4)
-        ln_out(last - 4)
+        ln_gain(last - 3)
+        ln_gain(last - 2)
         ln_sum(last)
         ln_squares(last)
         ln_rstd_scalar(last)
+        ln_negmean(last - 1)
         ln_negmean(last)
-        ln_gain(last - 3)
-        ln_out(last - 3)
-        ln_gain(last - 2)
-        ln_out(last - 2)
+        ln_out(last - 7)
+        ln_out(last - 6)
+        ln_out(last - 5)
         ln_gain(last - 1)
-        ln_out(last - 1)
+        ln_out(last - 4)
         ln_gain(last)
-        ln_out(last)
+        for e in (last - 3, last - 2, last - 1, last):
+            ln_out(e)

@@ -32,7 +32,7 @@ PE_PART = H // 2
 
 
 def split(r):
-    return 88 if r < OUT_FROM else 224
+    return 104 if r < OUT_FROM else 240
 
 
 def regroup(copy, dst, src):
@@ -310,7 +310,7 @@ def tile_structuralequationmodels_kernel(
             T[("tt", e)] = tt
 
         def ln_out(e):
-            o = lnp.tile([P, BC, V], F32, name="o")
+            o = lnp.tile([P, BC, V], F32, name="o", bufs=8)
             for bc in range(BC):
                 nc.vector.scalar_tensor_tensor(
                     out=o[:, bc, :],

from contextlib import ExitStack

import concourse.mybir as mybir
from concourse.masks import make_identity

FP8X4 = mybir.dt.float8_e4m3fn_x4
BF16 = mybir.dt.bfloat16
F32 = mybir.dt.float32
U32 = mybir.dt.uint32
U8 = mybir.dt.uint8
ALU = mybir.AluOpType
ACT = mybir.ActivationFunctionType

B, D, V, H = 256, 16, 128, 512
K = D * V
P = 128
PACK = 4
K_PASS = P * PACK
G = K // K_PASS
C = H // P
BC = B // P
LN_EPS = 1e-5
FLOPS = 2 * B * D * (K * H + H * V)

AHEAD = 2
UA, UV, UB, UC = 0, 1, 2, 3
PASS_ORDER = (UA, UB, UV, UC)
EARLY_B2 = 4
OUT_FROM = 11
PE_FROM = 3
PE_PART = H // 2


def split(r):
    return 104 if r < OUT_FROM else 240


def regroup(copy, dst, src):
    copy(
        out=dst.rearrange("p (c i) t -> p c t i", i=4),
        in_=src.rearrange("p t (c i) -> p c t i", i=4),
    )


def group(e):
    if e < D // 2:
        return (0, D // 2 - 1)
    if e < D - 2:
        return (D // 2, D - 3)
    return (e, e)


def finished(r):
    return [e for e in range(D // 2) if OUT_FROM + e * (D - OUT_FROM) // (D // 2) == r]


def live(e):
    return 0 <= e < D


def tile_structuralequationmodels_kernel(
    tc, causal_vars, adj_soft, W1, b1, W2, b2, gamma, beta, out
):
    nc = tc.nc
    with ExitStack() as ctx:
        const = ctx.enter_context(tc.tile_pool(name="const", bufs=1))
        rawp = ctx.enter_context(tc.tile_pool(name="rawp", bufs=(AHEAD + 1) * G))
        grpp = ctx.enter_context(tc.tile_pool(name="grpp", bufs=6))
        w1qp = ctx.enter_context(tc.tile_pool(name="w1qp", bufs=3))
        xp = ctx.enter_context(tc.tile_pool(name="xp", bufs=2))
        xqp = ctx.enter_context(tc.tile_pool(name="xqp", bufs=3))
        hp = ctx.enter_context(tc.tile_pool(name="hp", bufs=3))
        lnp = ctx.enter_context(tc.tile_pool(name="lnp", bufs=3))
        stp = ctx.enter_context(tc.tile_pool(name="stp", bufs=4))
        ps_set = ctx.enter_context(tc.psum_pool(name="ps_set", bufs=2))
        ps_h = ctx.enter_context(tc.psum_pool(name="ps_h", bufs=1))
        ps_y = ctx.enter_context(tc.psum_pool(name="ps_y", bufs=2))
        ctx.enter_context(tc.manual_schedule())

        T = {}
        out_v = out.rearrange("(c p) i v -> p c i v", p=P)

        def load_w1(e, g):
            T[("raw", e, g)] = rawp.tile([P, PACK, H], BF16, name="raw")
            rows = W1[e][g * K_PASS : (g + 1) * K_PASS, :].rearrange("(p t) h -> p t h", t=PACK)
            nc.sync.dma_start(out=T[("raw", e, g)][:], in_=rows)

        def load_halves(g, n):
            if ("raw", 0, g) not in T:
                T[("raw", 0, g)] = rawp.tile([P, 2, PACK, H // 2], BF16, name="raw2", tag="raw")
            rows = W1[0][g * K_PASS : (g + 1) * K_PASS, :].rearrange("(p t) h -> p t h", t=PACK)
            nc.sync.dma_start(out=T[("raw", 0, g)][:, n], in_=rows[:, :, n * H // 2 : (n + 1) * H // 2])

        def regroup_halves(g, n):
            if ("grp", 0, g) not in T:
                T[("grp", 0, g)] = grpp.tile([P, H, PACK], BF16, name="grp", align_bytes=64)
            dst = T[("grp", 0, g)][:, n * H // 2 : (n + 1) * H // 2, :]
            regroup(nc.scalar.copy, dst, T[("raw", 0, g)][:, n])

        def w1_regroup(e, g, copy, lo=0, hi=H):
            if hi <= lo:
                return
            if ("grp", e, g) not in T:
                T[("grp", e, g)] = grpp.tile([P, H, PACK], BF16, name="grp", align_bytes=64)
            regroup(copy, T[("grp", e, g)][:, lo:hi, :], T[("raw", e, g)][:, :, lo:hi])

        def pe_regroup(e):
            for n in range(2):
                bank = ps_set.tile([P, PE_PART, PACK], BF16, name="bank", tag="set")
                for m in range(2):
                    cols = slice(m * PE_PART // 2, (m + 1) * PE_PART // 2)
                    first = n * PE_PART + m * PE_PART // 2
                    nc.tensor.matmul(
                        out=bank[:, cols, :].rearrange("p h t -> p t h"),
                        lhsT=ident_b[:],
                        rhs=T[("raw", e, UC)][:, :, first : first + PE_PART // 2],
                        start=True,
                        stop=True,
                    )
                T[("bank", e, n)] = bank

        def pe_copy_out(e):
            grp = grpp.tile([P, H, PACK], BF16, name="grp", align_bytes=64)
            T[("grp", e, UC)] = grp
            for n in range(2):
                nc.scalar.copy(out=grp[:, n * PE_PART : (n + 1) * PE_PART, :], in_=T[("bank", e, n)][:])

        def w1_quant(e, g, lo=0, hi=H):
            if g == PASS_ORDER[0]:
                T[("w1c", e)] = w1qp.tile([P, G, H], U32, name="w1c", align_bytes=64)
                T[("w1s", e)] = w1qp.tile([P, G, H], U8, name="w1s", align_bytes=64)
            nc.vector.quantize_mx(
                out=T[("w1c", e)][:, g, lo:hi].bitcast(FP8X4),
                scales=T[("w1s", e)][:, g, lo:hi],
                in_=T[("grp", e, g)][:, lo:hi, :].rearrange("p w t -> p (w t)"),
            )

        def x_scale(e, passes=range(G)):
            if ("xs", e) not in T:
                T[("xs", e)] = xp.tile([P, G, B * PACK], BF16, name="xs", align_bytes=64)
            for g in passes:
                nc.vector.tensor_scalar(
                    out=T[("xs", e)][:, g, :],
                    in0=cvg[:, g].rearrange("p b t -> p (b t)"),
                    scalar1=adjcol[:, G * e + g : G * e + g + 1],
                    scalar2=None,
                    op0=ALU.mult,
                )

        def x_quant(e, lo=0, hi=G):
            if ("xc", e) not in T:
                T[("xc", e)] = xqp.tile([P, G * B], U32, name="xc", align_bytes=64)
                T[("xsc", e)] = xqp.tile([P, G * B], U8, name="xsc", align_bytes=64)
            nc.vector.quantize_mx(
                out=T[("xc", e)][:, lo * B : hi * B].bitcast(FP8X4),
                scales=T[("xsc", e)][:, lo * B : hi * B],
                in_=T[("xs", e)][:, lo:hi, :].rearrange("p g e -> p (g e)"),
            )

        def mm1(e, g, chunks=range(C)):
            first = g == PASS_ORDER[0]
            last = g == PASS_ORDER[-1]
            for c in chunks:
                if first:
                    T[("hps", e, c)] = ps_h.tile([P, B], F32, name="hps%d" % c)
                nc.tensor.matmul_mx(
                    out=T[("hps", e, c)][:],
                    lhsT=T[("w1c", e)][:, g, c * P : (c + 1) * P].bitcast(FP8X4),
                    lhsT_scale=T[("w1s", e)][:, g, c * P : (c + 1) * P],
                    rhs=T[("xc", e)][:, g * B : (g + 1) * B].bitcast(FP8X4),
                    rhs_scale=T[("xsc", e)][:, g * B : (g + 1) * B],
                    start=first,
                    stop=last,
                )

        def gelu(e, chunks=range(C), lo=0, hi=B):
            if ("ht", e, lo) not in T:
                T[("ht", e, lo)] = hp.tile([P, C, hi - lo], BF16, name="ht")
            for c in chunks:
                nc.scalar.activation(
                    out=T[("ht", e, lo)][:, c, :],
                    in_=T[("hps", e, c)][:, lo:hi],
                    func=ACT.Gelu,
                    bias=b1col[:, C * e + c : C * e + c + 1],
                    scale=1.0,
                )

        def h_regroup(e, copy, lo=0, hi=B):
            if ("hg", e) not in T:
                T[("hg", e)] = hp.tile([P, B, PACK], BF16, name="hg", align_bytes=64)
            regroup(copy, T[("hg", e)][:, lo:hi, :], T[("ht", e, lo)][:])

        def h_quant(e, lo=0, hi=B):
            if ("hc", e) not in T:
                T[("hc", e)] = hp.tile([P, B], U32, name="hc", align_bytes=64)
                T[("hs", e)] = hp.tile([P, B], U8, name="hs", align_bytes=64)
            nc.vector.quantize_mx(
                out=T[("hc", e)][:, lo:hi].bitcast(FP8X4),
                scales=T[("hs", e)][:, lo:hi],
                in_=T[("hg", e)][:, lo:hi, :].rearrange("p w t -> p (w t)"),
            )

        def w2_regroup(e):
            g2 = hp.tile([P, 2 * V, PACK], BF16, name="g2", align_bytes=64)
            src = w2r[e // 4][:, :, e % 4 : e % 4 + 2, :]
            regroup(nc.vector.tensor_copy, g2[:], src.rearrange("p t i v -> p t (i v)"))
            T[("g2", e)] = g2

        def w2_quant(e):
            w2c = hp.tile([P, 2 * V], U32, name="w2c", align_bytes=64)
            w2s = hp.tile([P, 2 * V], U8, name="w2s", align_bytes=64)
            nc.vector.quantize_mx(
                out=w2c[:].bitcast(FP8X4),
                scales=w2s[:],
                in_=T[("g2", e)][:].rearrange("p w t -> p (w t)"),
            )
            for m in range(2):
                T[("w2c", e + m)] = w2c[:, m * V : (m + 1) * V]
                T[("w2s", e + m)] = w2s[:, m * V : (m + 1) * V]

        def mm2(e):
            yps = ps_y.tile([P, BC, V], F32, name="yps", tag="yps")
            for bc in range(BC):
                nc.tensor.matmul_mx(
                    out=yps[:, bc, :],
                    lhsT=T[("hc", e)][:, bc * P : (bc + 1) * P].bitcast(FP8X4),
                    lhsT_scale=T[("hs", e)][:, bc * P : (bc + 1) * P],
                    rhs=T[("w2c", e)].bitcast(FP8X4),
                    rhs_scale=T[("w2s", e)],
                    start=True,
                    stop=True,
                )
            T[("yps", e)] = yps

        def ln_sum(e):
            first, last = group(e)
            if e == first:
                T[("sz", first)] = stp.tile([P, (last - first + 1) * BC], F32, name="sz")
            z = lnp.tile([P, BC, V], F32, name="z", bufs=10)
            for bc in range(BC):
                at = (e - first) * BC + bc
                nc.vector.scalar_tensor_tensor(
                    out=z[:, bc, :],
                    in0=T[("yps", e)][:, bc, :],
                    scalar=1.0,
                    in1=b2bc[:, e * V : (e + 1) * V],
                    op0=ALU.mult,
                    op1=ALU.add,
                    accum_out=T[("sz", first)][:, at : at + 1],
                )
            T[("z", e)] = z

        def ln_negmean(e):
            first, last = group(e)
            nm = stp.tile([P, (last - first + 1) * BC], F32, name="nm")
            nc.vector.tensor_scalar(
                out=nm[:], in0=T[("sz", first)][:], scalar1=-1.0 / V, scalar2=None, op0=ALU.mult
            )
            for m in range(first, last + 1):
                T[("nm", m)] = nm[:, (m - first) * BC : (m - first + 1) * BC]

        def ln_squares(e):
            first, last = group(e)
            if e == first:
                T[("ssq", first)] = stp.tile([P, (last - first + 1) * BC], F32, name="ssq")
            for bc in range(BC):
                junk = lnp.tile([P, V], F32, name="junk")
                at = (e - first) * BC + bc
                nc.scalar.activation(
                    out=junk[:],
                    in_=T[("z", e)][:, bc, :],
                    func=ACT.Square,
                    bias=T[("sz", first)][:, at : at + 1],
                    scale=-float(V),
                    accum_out=T[("ssq", first)][:, at : at + 1],
                )

        def ln_rstd(e):
            first, last = group(e)
            width = (last - first + 1) * BC
            ve = stp.tile([P, width], F32, name="ve")
            nc.vector.tensor_scalar(
                out=ve[:], in0=T[("ssq", first)][:], scalar1=1.0 / V**3, scalar2=LN_EPS, op0=ALU.mult, op1=ALU.add
            )
            rstd = stp.tile([P, width], F32, name="rstd")
            nc.gpsimd.tensor_tensor(out=rstd[:], in0=ve[:], in1=negh[:, 0:width], op=ALU.pow)
            for m in range(first, last + 1):
                T[("rstd", m)] = rstd[:, (m - first) * BC : (m - first + 1) * BC]

        def ln_rstd_scalar(e):
            first, last = group(e)
            rstd = stp.tile([P, (last - first + 1) * BC], F32, name="rstd1")
            nc.scalar.activation(
                out=rstd[:], in_=T[("ssq", first)][:], func=ACT.Abs_reciprocal_sqrt, bias=LN_EPS, scale=1.0 / V**3
            )
            for m in range(first, last + 1):
                T[("rstd", m)] = rstd[:, (m - first) * BC : (m - first + 1) * BC]

        def ln_gain(e):
            tt = lnp.tile([P, BC, V], F32, name="tt", bufs=6)
            for bc in range(BC):
                nc.vector.scalar_tensor_tensor(
                    out=tt[:, bc, :],
                    in0=T[("z", e)][:, bc, :],
                    scalar=T[("nm", e)][:, bc : bc + 1],
                    in1=gbc[:, e * V : (e + 1) * V],
                    op0=ALU.add,
                    op1=ALU.mult,
                )
            T[("tt", e)] = tt

        def ln_out(e):
            o = lnp.tile([P, BC, V], F32, name="o", bufs=8)
            for bc in range(BC):
                nc.vector.scalar_tensor_tensor(
                    out=o[:, bc, :],
                    in0=T[("tt", e)][:, bc, :],
                    scalar=T[("rstd", e)][:, bc : bc + 1],
                    in1=bbc[:, e * V : (e + 1) * V],
                    op0=ALU.mult,
                    op1=ALU.add,
                )
            nc.sync.dma_start(out=out_v[:, :, e, :], in_=o[:])

        cv_v = causal_vars.rearrange("(c p) j v -> p c (j v)", p=P)
        cvr = [const.tile([P, BC, K_PASS], BF16, name="cvr%d" % g) for g in range(G)]
        ones_b = const.tile([P, P], BF16, name="ones_b")
        rowt = const.tile([P, D * D + EARLY_B2 * V], BF16, name="rowt")
        b1t = const.tile([P, P], BF16, name="b1t")
        w2r = [const.tile([P, PACK, 4, V], BF16, name="w2r%d" % q) for q in range(D // 4)]
        b2bc = const.tile([P, D * V], BF16, name="b2bc")
        gbc = const.tile([P, D * V], BF16, name="gbc")
        bbc = const.tile([P, D * V], BF16, name="bbc")
        nc.vector.memset(rowt[:], 0.0)
        nc.vector.memset(ones_b[:], 1.0)
        nc.vector.memset(b1t[:], 0.0)

        def load_w2(q):
            for t in range(PACK):
                nc.sync.dma_start(
                    out=w2r[q][:, t],
                    in_=W2[4 * q : 4 * q + 4, t * P : (t + 1) * P, :].rearrange("i p v -> p i v"),
                )

        def load_x(g):
            cols = slice(g * K_PASS, (g + 1) * K_PASS)
            nc.sync.dma_start(out=cvr[g][:], in_=cv_v[:, :, cols])

        load_x(0)
        load_halves(UA, 0)
        nc.sync.dma_start(out=rowt[0:1, 0 : D * D], in_=adj_soft.rearrange("(o i) j -> o (i j)", o=1))
        load_x(1)
        load_halves(UA, 1)
        load_x(2)
        load_halves(UB, 0)
        load_x(3)
        load_halves(UB, 1)
        load_w1(0, UC)
        load_w1(0, UV)
        nc.sync.dma_start(out=b1t[0 : D * C, :], in_=b1.rearrange("i (c m) -> (i c) m", m=P))
        nc.sync.dma_start(
            out=rowt[0:1, D * D :], in_=b2[0:EARLY_B2].rearrange("(o i) v -> o (i v)", o=1)
        )
        load_w1(1, UA)
        load_w1(1, UB)
        load_w1(1, UV)
        load_w2(0)
        load_w1(1, UC)

        def load_spread(r):
            if r == 2:
                nc.sync.dma_start(
                    out=b2bc[:, EARLY_B2 * V :],
                    in_=b2[EARLY_B2:D].rearrange("i v -> (i v)").partition_broadcast(P),
                )
            if r == 3:
                nc.sync.dma_start(out=gbc[:], in_=gamma.rearrange("i v -> (i v)").partition_broadcast(P))
            if r == 4:
                nc.sync.dma_start(out=bbc[:], in_=beta.rearrange("i v -> (i v)").partition_broadcast(P))

        ident_f = const.tile([P, P], F32, name="ident_f")
        make_identity(nc, ident_f[:])
        ident_b = const.tile([P, P], BF16, name="ident_b")
        make_identity(nc, ident_b[:])
        negh = const.tile([P, D // 2 * BC], F32, name="negh")
        nc.vector.memset(negh[:], -0.5)
        warm = const.tile([P, 1], F32, name="warm")
        nc.scalar.activation(out=warm[:], in_=negh[:, 0:1], func=ACT.Gelu)
        adjcol = const.tile([P, D * G], F32, name="adjcol")
        b1col = const.tile([P, D * C], F32, name="b1col")
        cvg = const.tile([P, G, B, PACK], BF16, name="cvg", align_bytes=64)

        def x_turn(g):
            cvw = cvr[g][:].bitcast(F32)
            xt = ps_set.tile([P, 2, B], F32, name="xt", tag="set")
            for bc in range(BC):
                for u in range(2):
                    nc.tensor.transpose(
                        xt[:, u, bc * P : (bc + 1) * P],
                        cvw[:, bc, u::2],
                        ident_f[:],
                    )
            T[("xt", g)] = xt

        def x_copy(g):
            cvgw = cvg[:].bitcast(F32)
            nc.vector.tensor_copy(out=cvgw[:, g], in_=T[("xt", g)][:].rearrange("p u b -> p b u"))

        def adj_spread():
            adj_ps = ps_set.tile([P, D * D], F32, name="adj_ps", tag="set")
            nc.tensor.matmul(out=adj_ps[:], lhsT=ones_b[:], rhs=rowt[:, 0 : D * D], start=True, stop=True)
            for q in range(4):
                rows = slice(32 * q, 32 * q + 32)
                nc.vector.tensor_copy(
                    out=adjcol[rows, :].rearrange("p (i g) -> p i g", g=G),
                    in_=adj_ps[rows, :].rearrange("p (i g q) -> p i g q", g=G, q=4)[:, :, :, q],
                )

        def bias_spread():
            b1ps = ps_set.tile([P, P], BF16, name="b1ps", tag="set")
            nc.tensor.transpose(b1ps[:], b1t[:], ident_b[:])
            nc.vector.tensor_copy(out=b1col[:], in_=b1ps[:, 0 : D * C])
            b2_ps = ps_y.tile([P, EARLY_B2 * V], F32, name="b2_ps", tag="yps")
            nc.tensor.matmul(out=b2_ps[:], lhsT=ones_b[:], rhs=rowt[:, D * D :], start=True, stop=True)
            T[("b2_ps", 0)] = b2_ps

        s_copy = nc.scalar.copy
        v_copy = nc.vector.tensor_copy

        for g in range(G):
            load_w1(AHEAD, g)
        for n in range(2):
            regroup_halves(UA, n)
        for n in range(2):
            regroup_halves(UB, n)
        w1_regroup(0, UC, s_copy)
        x_turn(0)
        x_copy(0)
        adj_spread()
        x_turn(1)
        x_scale(0, (0,))
        x_copy(1)
        x_quant(0, 0, 1)
        x_scale(0, (1,))
        x_turn(2)
        w1_quant(0, UA)
        x_copy(2)
        x_quant(0, 1, 2)
        x_scale(0, (2,))
        x_turn(3)
        x_copy(3)
        x_quant(0, 2, 3)
        x_scale(0, (3,))
        w1_quant(0, UB)
        x_quant(0, 3, 4)
        mm1(0, UA)
        mm1(0, UB)
        w1_regroup(0, UV, v_copy)
        bias_spread()
        w1_quant(0, UV)
        mm1(0, UV)

        for r in range(1, D):
            e0, e1, e2, e3 = r, r - 1, r - 2, r - 3
            sv = split(r)
            if live(e0 + AHEAD):
                for g in range(G):
                    load_w1(e0 + AHEAD, g)
                if e0 <= 3:
                    load_w2(e0)
                load_spread(e0)
            if live(e2):
                h_quant(e2)
                mm2(e2)
            w1_quant(e1, UC)
            mm1(e1, UC)
            if e0 >= PE_FROM:
                pe_regroup(e0)
            w1_regroup(e0, UA, s_copy)
            x_scale(e0)
            if live(e3) and e3 == group(e3)[1]:
                ln_negmean(e3)
                ln_rstd(e3)
            if live(e2):
                ln_sum(e2)
            w1_regroup(e0, UB, s_copy)
            gelu(e1)
            w1_quant(e0, UA)
            x_quant(e0)
            mm1(e0, UA)
            w1_regroup(e0, UV, s_copy, 0, sv)
            w1_regroup(e0, UV, v_copy, sv, H)
            if e0 >= PE_FROM:
                pe_copy_out(e0)
            else:
                w1_regroup(e0, UC, s_copy)
            w1_quant(e0, UB)
            if e0 == 1:
                nc.scalar.copy(out=b2bc[:, 0 : EARLY_B2 * V], in_=T[("b2_ps", 0)][:])
            mm1(e0, UB)
            if live(e2):
                ln_squares(e2)
            for e in finished(r):
                ln_gain(e)
            w1_quant(e0, UV)
            mm1(e0, UV)
            h_regroup(e1, v_copy)
            pair = 0 if e0 == 1 else e0
            if pair % 2 == 0:
                w2_regroup(pair)
            for e in finished(r):
                ln_out(e)
            if pair % 2 == 0:
                w2_quant(pair)

        last = D - 1
        for n in range(2):
            w1_quant(last, UC, n * H // 2, (n + 1) * H // 2)
            mm1(last, UC, range(2 * n, 2 * n + 2))
        for chunks in (range(0, 2), range(2, 4)):
            for bc in range(BC):
                gelu(last, chunks, bc * P, (bc + 1) * P)
        h_quant(last - 1)
        mm2(last - 1)
        ln_negmean(last - 2)
        ln_gain(last - 7)
        ln_gain(last - 6)
        h_regroup(last, v_copy, 0, P)
        h_regroup(last, s_copy, P, B)
        nc.scalar.activation(out=warm[:], in_=negh[:, 0:1], func=ACT.Abs_reciprocal_sqrt)
        ln_rstd_scalar(last - 2)
        ln_sum(last - 1)
        ln_squares(last - 1)
        ln_rstd_scalar(last - 1)
        ln_gain(last - 5)
        for bc in range(BC):
            h_quant(last, bc * P, (bc + 1) * P)
        mm2(last)
        ln_gain(last - 4)
        ln_gain(last - 3)
        ln_gain(last - 2)
        ln_sum(last)
        ln_squares(last)
        ln_rstd_scalar(last)
        ln_negmean(last - 1)
        ln_negmean(last)
        ln_out(last - 7)
        ln_out(last - 6)
        ln_out(last - 5)
        ln_gain(last - 1)
        ln_out(last - 4)
        ln_gain(last)
        for e in (last - 3, last - 2, last - 1, last):
            ln_out(e)
